import numpy as np
import ml_dtypes


def mxq(x, axis, fmt="e4m3"):
    dtype, down = {"e4m3": (ml_dtypes.float8_e4m3fn, 7), "e5m2": (ml_dtypes.float8_e5m2, 14)}[fmt]
    v = np.moveaxis(np.asarray(x, np.float32).astype(ml_dtypes.bfloat16).astype(np.float64), axis, -1)
    blocks = v.reshape(v.shape[:-1] + (-1, 32))
    amax = np.abs(blocks).max(-1, keepdims=True)
    byte = np.maximum(np.where(amax > 0, np.frexp(amax)[1] - 1 + 127, 0) - down, 1)
    scale = np.exp2(byte - 127.0)
    codes = (blocks / scale).astype(np.float32).astype(dtype).astype(np.float64)
    return np.moveaxis((codes * scale).reshape(v.shape), -1, axis)


WIDE = False


def mx_kscale(k):
    if not WIDE:
        return np.ones(k)
    levels = np.array([10, -10, 5, -5, 0])
    a = np.random.permutation(np.resize(levels, k // 512 * 4)).reshape(k // 512, 4)
    idx = np.arange(k)
    return np.exp2(a[idx // 512, idx % 128 // 32])


BF16 = ml_dtypes.bfloat16


def bf(x):
    return np.asarray(x, np.float32).astype(BF16)


def f64(x):
    return np.asarray(x).astype(np.float64)


E2M1 = np.array([0.0, 0.5, 1.0, 1.5, 2.0, 3.0, 4.0, 6.0, -0.0, -0.5, -1.0, -1.5, -2.0, -3.0, -4.0, -6.0])


def pack_weight(w, fmt):
    k, n = w.shape
    w = f64(bf(w)).reshape(k // 32, 32, n)
    amax = np.abs(w).max(1)
    if fmt == "e4m3":
        byte = np.frexp(amax)[1] - 1 + 127 - 7
    else:
        mant, ex = np.frexp(amax / 6.0)
        byte = np.where(mant > 0.5, ex, ex - 1) + 127
    byte = np.clip(np.where(amax > 0, byte, 1), 1, 254)
    scaled = (w * np.exp2(127.0 - byte)[:, None, :]).reshape(k, n).astype(np.float32)
    by_word = np.ascontiguousarray(scaled.reshape(k // 512, 128, 4, n).transpose(0, 1, 3, 2))
    if fmt == "e4m3":
        words = by_word.astype(ml_dtypes.float8_e4m3fn).view(np.uint8)
    else:
        c = by_word.astype(ml_dtypes.float4_e2m1fn).view(np.uint8) & 0xF
        words = c[..., 0::2] | (c[..., 1::2] << 4)
    return np.ascontiguousarray(words), np.ascontiguousarray(byte.astype(np.uint8).reshape(k // 512, 16, n))


def unpack_weight(words, scales, fmt):
    g, p, n, _ = words.shape
    if fmt == "e4m3":
        vals = np.ascontiguousarray(words).view(ml_dtypes.float8_e4m3fn).astype(np.float64)
    else:
        nib = np.empty((g, p, n, 4), np.uint8)
        nib[..., 0::2] = words & 0xF
        nib[..., 1::2] = words >> 4
        vals = E2M1[nib]
    vals = vals * np.repeat(np.exp2(scales.astype(np.float64) - 127.0), 8, axis=1)[..., None]
    return vals.transpose(0, 1, 3, 2).reshape(g * 512, n)


B, H, HD = 4096, 2, 512
W = H * HD


def sigmoid(v):
    return 1.0 / (1.0 + np.exp(-v))


def softplus(v):
    return np.log(1.0 + np.exp(v))


def block_diag_linear(xq, w, b):
    y = (xq.transpose(1, 0, 2) @ w).transpose(1, 0, 2) + f64(b)
    return y.reshape(B, W)


def setup_inputs():
    s = mx_kscale(W)
    s = s / s.max()
    sw = s.reshape(H, HD, 1)
    x = bf(np.random.standard_normal((B, W)) * s)
    state = bf(np.random.standard_normal((B, W)))
    w_in = np.random.standard_normal((H, HD, HD)) / np.sqrt(HD) / sw
    w_in_words, w_in_scales = pack_weight(w_in.reshape(-1, HD), "e4m3")
    b_in = bf(np.random.standard_normal((H, HD)) * 0.5)
    w_a = np.random.standard_normal((H, HD, HD)) / np.sqrt(HD) / sw
    w_a_words, w_a_scales = pack_weight(w_a.reshape(-1, HD), "e4m3")
    b_a = bf(np.random.standard_normal((H, HD)) * 0.5)
    a_param = bf(-2.0 + 0.5 * np.random.standard_normal(W))
    return {"x": x,
            "state": state,
            "w_in_words": w_in_words,
            "w_in_scales": w_in_scales,
            "b_in": b_in,
            "w_a_words": w_a_words,
            "w_a_scales": w_a_scales,
            "b_a": b_a,
            "a_param": a_param}


def reference(x, state, w_in_words, w_in_scales, b_in, w_a_words, w_a_scales, b_a, a_param):
    xq = mxq(f64(x).reshape(B, H, HD), 2, "e4m3")
    gate_x = sigmoid(block_diag_linear(xq, unpack_weight(w_in_words, w_in_scales, "e4m3").reshape(H, HD, HD), b_in))
    gate_a = sigmoid(block_diag_linear(xq, unpack_weight(w_a_words, w_a_scales, "e4m3").reshape(H, HD, HD), b_a))
    log_a = -8.0 * gate_a * softplus(f64(a_param))
    a = np.exp(log_a)
    scale = np.sqrt(1.0 - np.exp(2.0 * log_a))
    return a * f64(state) + gate_x * f64(x) * scale

@@ -1,0 +1,242 @@
+from contextlib import ExitStack
+
+import concourse.mybir as mybir
+from concourse.masks import make_identity
+
+F32 = mybir.dt.float32
+BF16 = mybir.dt.bfloat16
+I32 = mybir.dt.int32
+U32 = mybir.dt.uint32
+U8 = mybir.dt.uint8
+FP8X4 = mybir.dt.float8_e4m3fn_x4
+ACT = mybir.ActivationFunctionType
+ALU = mybir.AluOpType
+
+P = 128
+PACK = 4
+ROWS = 4096
+HEADS = 2
+HEAD = 512
+CHANNELS = HEADS * HEAD
+BLOCK = 512
+BLOCKS = ROWS // BLOCK
+ROW_TILES = BLOCK // P
+CHANNEL_TILES = HEAD // P
+GATE_X, GATE_A = 0, 1
+ROOT_TILES = 2
+
+FLOPS = 2 * ROWS * HEAD * HEAD * HEADS * 2
+
+
+def tile_rglru_t_e_kernel(
+    tc, x, state, w_in_words, w_in_scales, b_in, w_a_words, w_a_scales, b_a, a_param, out
+):
+    nc = tc.nc
+    x_blocks = x.rearrange("(b p t) c -> b p t c", p=P, t=ROW_TILES)
+    state_blocks = state.rearrange("(b p t) c -> b p t c", p=P, t=ROW_TILES)
+    out_blocks = out.rearrange("(b p t) c -> b p t c", p=P, t=ROW_TILES)
+
+    with ExitStack() as ctx:
+        keep = ctx.enter_context(tc.tile_pool(name="keep", bufs=1))
+        x_pool = ctx.enter_context(tc.tile_pool(name="x", bufs=3))
+        state_pool = ctx.enter_context(tc.tile_pool(name="state", bufs=2))
+        quant_pool = ctx.enter_context(tc.tile_pool(name="quant", bufs=HEADS))
+        gate_pool = ctx.enter_context(tc.tile_pool(name="gate", bufs=HEADS + 1))
+        root_pool = ctx.enter_context(tc.tile_pool(name="root", bufs=HEADS))
+        out_pool = ctx.enter_context(tc.tile_pool(name="out", bufs=4))
+        sum_pool = ctx.enter_context(tc.psum_pool(name="sums", bufs=4))
+        turn_pool = ctx.enter_context(tc.psum_pool(name="turned", bufs=4))
+        ctx.enter_context(tc.manual_schedule())
+
+        x_of, state_of = {}, {}
+        grouped_of, codes_of, planes_of = {}, {}, {}
+        a_of, g_of, root_of = {}, {}, {}
+
+        def load_x(b):
+            x_sb = x_pool.tile([P, ROW_TILES, CHANNELS], BF16)
+            nc.sync.dma_start(out=x_sb[:], in_=x_blocks[b])
+            x_of[b] = x_sb
+
+        def load_state(b):
+            state_sb = state_pool.tile([P, ROW_TILES, CHANNELS], BF16)
+            nc.sync.dma_start(out=state_sb[:], in_=state_blocks[b])
+            state_of[b] = state_sb
+
+        ident = keep.tile([P, P], F32)
+        make_identity(nc, ident[:])
+        w_planes = keep.tile([P, 2 * HEADS, HEAD], U8, align_bytes=64)
+        nc.vector.memset(w_planes[:].bitcast(I32), 0)
+        vector_rows = keep.tile([P, P], BF16)
+        nc.vector.memset(vector_rows[:], 0.0)
+        quarter = keep.tile([P, 1], F32)
+        nc.vector.memset(quarter[:], 0.25)
+        one = keep.tile([P, 1], F32)
+        nc.vector.memset(one[:], 1.0)
+
+        nc.sync.dma_start(out=vector_rows[0:8, :], in_=b_in.rearrange("h (m p) -> (h m) p", p=P))
+        nc.sync.dma_start(out=vector_rows[8:16, :], in_=b_a.rearrange("h (m p) -> (h m) p", p=P))
+        nc.sync.dma_start(out=vector_rows[16:24, :], in_=a_param.rearrange("(m p) -> m p", p=P))
+        load_x(0)
+        w_codes = keep.tile([P, 2 * HEADS, HEAD], I32, align_bytes=64)
+        for gate, words in ((GATE_X, w_in_words), (GATE_A, w_a_words)):
+            nc.sync.dma_start(
+                out=w_codes[:, HEADS * gate : HEADS * (gate + 1), :],
+                in_=words.rearrange("g p n t -> p g (n t)").bitcast(I32),
+            )
+        for gate, scales in ((GATE_X, w_in_scales), (GATE_A, w_a_scales)):
+            for quadrant in range(4):
+                nc.sync.dma_start(
+                    out=w_planes[
+                        32 * quadrant : 32 * quadrant + 4, HEADS * gate : HEADS * (gate + 1), :
+                    ].bitcast(I32),
+                    in_=scales[:, 4 * quadrant : 4 * quadrant + 4, :]
+                    .rearrange("g r n -> r g n")
+                    .bitcast(I32),
+                )
+
+        vector_f32 = keep.tile([P, P], F32)
+        nc.vector.tensor_copy(out=vector_f32[:], in_=vector_rows[:])
+        vector_cols = turn_pool.tile([P, HEAD], F32, tag="turned")
+        nc.tensor.transpose(vector_cols[:, 0:P], vector_f32[:], ident[:])
+        half_bias = keep.tile([P, 16], F32)
+        nc.vector.tensor_scalar_mul(out=half_bias[:], in0=vector_cols[:, 0:16], scalar1=0.5)
+        a_par = keep.tile([P, 8], F32)
+        nc.vector.tensor_copy(out=a_par[:], in_=vector_cols[:, 16:24])
+        soft = keep.tile([P, 8], F32)
+        nc.scalar.activation(out=soft[:], in_=a_par[:], func=ACT.Abs)
+        nc.scalar.activation(out=soft[:], in_=soft[:], func=ACT.Exp, scale=-1.0)
+        nc.scalar.activation(out=soft[:], in_=soft[:], func=ACT.Ln, bias=one[:])
+
+        def regroup(b, h):
+            x_words = x_of[b][:].bitcast(F32)
+            grouped = quant_pool.tile([P, BLOCK, PACK], BF16, align_bytes=64)
+            grouped_words = grouped[:].bitcast(F32)
+            for pair in range(ROW_TILES // 2):
+                turned = turn_pool.tile([P, 2, 2, P], F32, tag="turned")
+                for i in range(2):
+                    for w in range(2):
+                        nc.tensor.transpose(
+                            turned[:, i, w, :],
+                            x_words[:, 2 * pair + i, 256 * h + w : 256 * (h + 1) : 2],
+                            ident[:],
+                        )
+                nc.vector.tensor_copy(
+                    out=grouped_words[:, 2 * P * pair : 2 * P * (pair + 1), :].rearrange(
+                        "p (i r) w -> p i r w", i=2
+                    ),
+                    in_=turned[:].rearrange("p i w r -> p i r w"),
+                )
+            grouped_of[b, h] = grouped
+
+        def quantise(b, h):
+            codes = quant_pool.tile([P, BLOCK], U32, align_bytes=64)
+            plane = quant_pool.tile([P, BLOCK], U8, align_bytes=64)
+            nc.vector.quantize_mx(
+                out=codes[:].bitcast(FP8X4),
+                scales=plane[:],
+                in_=grouped_of[b, h][:].rearrange("p r t -> p (r t)"),
+            )
+            codes_of[b, h], planes_of[b, h] = codes, plane
+
+        def open_unit(b, h):
+            a_t = gate_pool.tile([P, CHANNEL_TILES, BLOCK], F32)
+            g_t = gate_pool.tile([P, CHANNEL_TILES, BLOCK], F32)
+            root_t = root_pool.tile([P, CHANNEL_TILES, BLOCK], F32)
+            a_of[b, h], g_of[b, h], root_of[b, h] = a_t, g_t, root_t
+
+        def gates(b, h, m):
+            channels = slice(P * m, P * (m + 1))
+            column = CHANNEL_TILES * h + m
+            sums = {}
+            for gate in (GATE_A, GATE_X):
+                acc = sum_pool.tile([P, BLOCK], F32)
+                nc.tensor.matmul_mx(
+                    out=acc[:],
+                    lhsT=w_codes[:, HEADS * gate + h, channels].bitcast(FP8X4),
+                    lhsT_scale=w_planes[:, HEADS * gate + h, channels],
+                    rhs=codes_of[b, h][:].bitcast(FP8X4),
+                    rhs_scale=planes_of[b, h][:],
+                    start=True,
+                    stop=True,
+                )
+                sums[gate] = acc
+            a_part = a_of[b, h][:, m, :]
+            for gate, target in ((GATE_A, a_part), (GATE_X, g_of[b, h][:, m, :])):
+                nc.scalar.activation(
+                    out=target,
+                    in_=sums[gate][:],
+                    func=ACT.Tanh,
+                    bias=half_bias[:, 8 * gate + column : 8 * gate + column + 1],
+                    scale=0.5,
+                )
+            nc.scalar.activation(
+                out=a_part,
+                in_=a_part,
+                func=ACT.Exp,
+                bias=minus_4c[:, column : column + 1],
+                scale=minus_4c[:, column : column + 1],
+            )
+            nc.gpsimd.tensor_tensor(out=root_of[b, h][:, m, :], in0=a_part, in1=a_part, op=ALU.mult)
+
+        def roots(b, h):
+            for first in range(0, CHANNEL_TILES, ROOT_TILES):
+                root_part = root_of[b, h][:, first : first + ROOT_TILES, :]
+                g_part = g_of[b, h][:, first : first + ROOT_TILES, :]
+                nc.scalar.activation(
+                    out=root_part, in_=root_part, func=ACT.Sqrt, bias=quarter[:], scale=-0.25
+                )
+                nc.vector.scalar_tensor_tensor(
+                    out=g_part, in0=g_part, scalar=1.0, in1=root_part, op0=ALU.add, op1=ALU.mult
+                )
+
+        def combine(b, h, t):
+            rows = slice(P * t, P * (t + 1))
+            channels = slice(HEAD * h, HEAD * (h + 1))
+            turned_of = {}
+            for factor, source in (("a", a_of[b, h]), ("g", g_of[b, h])):
+                turned = turn_pool.tile([P, HEAD], F32, tag="turned")
+                for m in range(CHANNEL_TILES):
+                    nc.tensor.transpose(turned[:, P * m : P * (m + 1)], source[:, m, rows], ident[:])
+                turned_of[factor] = turned
+            result = out_pool.tile([P, HEAD], F32)
+            nc.vector.tensor_tensor(
+                out=result[:], in0=turned_of["a"][:], in1=state_of[b][:, t, channels], op=ALU.mult
+            )
+            fresh = out_pool.tile([P, HEAD], F32)
+            nc.vector.tensor_tensor(
+                out=fresh[:], in0=turned_of["g"][:], in1=x_of[b][:, t, channels], op=ALU.mult
+            )
+            nc.gpsimd.tensor_tensor(out=result[:], in0=result[:], in1=fresh[:], op=ALU.add)
+            nc.sync.dma_start(out=out_blocks[b][:, t, channels], in_=result[:])
+
+        for h in range(HEADS):
+            regroup(0, h)
+        for h in range(HEADS):
+            quantise(0, h)
+        nc.vector.scalar_tensor_tensor(
+            out=soft[:], in0=a_par[:], scalar=0.0, in1=soft[:], op0=ALU.max, op1=ALU.add
+        )
+        minus_4c = keep.tile([P, 8], F32)
+        nc.vector.tensor_scalar_mul(out=minus_4c[:], in0=soft[:], scalar1=-4.0)
+
+        for b in range(BLOCKS + 1):
+            if b + 1 < BLOCKS:
+                load_x(b + 1)
+            if b < BLOCKS:
+                load_state(b)
+            for h in range(HEADS):
+                if b < BLOCKS:
+                    open_unit(b, h)
+                for step in range(CHANNEL_TILES):
+                    if b < BLOCKS:
+                        gates(b, h, step)
+                    if b >= 1:
+                        combine(b - 1, h, step)
+            if b + 1 < BLOCKS:
+                for h in range(HEADS):
+                    regroup(b + 1, h)
+                for h in range(HEADS):
+                    quantise(b + 1, h)
+            if b < BLOCKS:
+                for h in range(HEADS):
+                    roots(b, h)

@@ -206,7 +206,7 @@ def tile_rglru_t_e_kernel(
             nc.vector.tensor_tensor(
                 out=fresh[:], in0=turned_of["g"][:], in1=x_of[b][:, t, channels], op=ALU.mult
             )
-            nc.gpsimd.tensor_tensor(out=result[:], in0=result[:], in1=fresh[:], op=ALU.add)
+            nc.vector.tensor_tensor(out=result[:], in0=result[:], in1=fresh[:], op=ALU.add)
             nc.sync.dma_start(out=out_blocks[b][:, t, channels], in_=result[:])
 
         for h in range(HEADS):

@@ -54,7 +54,9 @@ def tile_rglru_t_e_kernel(
 
         def load_x(b):
             x_sb = x_pool.tile([P, ROW_TILES, CHANNELS], BF16)
-            nc.sync.dma_start(out=x_sb[:], in_=x_blocks[b])
+            for h in range(HEADS):
+                channels = slice(HEAD * h, HEAD * (h + 1))
+                nc.sync.dma_start(out=x_sb[:, :, channels], in_=x_blocks[b][:, :, channels])
             x_of[b] = x_sb
 
         def load_state(b):
@@ -206,12 +208,12 @@ def tile_rglru_t_e_kernel(
             nc.vector.tensor_tensor(
                 out=fresh[:], in0=turned_of["g"][:], in1=x_of[b][:, t, channels], op=ALU.mult
             )
-            nc.vector.tensor_tensor(out=result[:], in0=result[:], in1=fresh[:], op=ALU.add)
+            adder = nc.gpsimd if h == 0 else nc.vector
+            adder.tensor_tensor(out=result[:], in0=result[:], in1=fresh[:], op=ALU.add)
             nc.sync.dma_start(out=out_blocks[b][:, t, channels], in_=result[:])
 
         for h in range(HEADS):
             regroup(0, h)
-        for h in range(HEADS):
             quantise(0, h)
         nc.vector.scalar_tensor_tensor(
             out=soft[:], in0=a_par[:], scalar=0.0, in1=soft[:], op0=ALU.max, op1=ALU.add

@@ -24,6 +24,9 @@ ROW_TILES = BLOCK // P
 CHANNEL_TILES = HEAD // P
 GATE_X, GATE_A = 0, 1
 ROOT_TILES = 2
+UNITS = BLOCKS * HEADS
+ROUND_UNITS = 4
+X_BLOCKS = ROUND_UNITS // HEADS + 2
 
 FLOPS = 2 * ROWS * HEAD * HEAD * HEADS * 2
 
@@ -38,12 +41,15 @@ def tile_rglru_t_e_kernel(
 
     with ExitStack() as ctx:
         keep = ctx.enter_context(tc.tile_pool(name="keep", bufs=1))
-        x_pool = ctx.enter_context(tc.tile_pool(name="x", bufs=3))
+        x_pool = ctx.enter_context(tc.tile_pool(name="x", bufs=X_BLOCKS))
         state_pool = ctx.enter_context(tc.tile_pool(name="state", bufs=2))
-        quant_pool = ctx.enter_context(tc.tile_pool(name="quant", bufs=HEADS))
-        gate_pool = ctx.enter_context(tc.tile_pool(name="gate", bufs=HEADS + 1))
-        root_pool = ctx.enter_context(tc.tile_pool(name="root", bufs=HEADS))
-        out_pool = ctx.enter_context(tc.tile_pool(name="out", bufs=4))
+        grouped_pool = ctx.enter_context(tc.tile_pool(name="grouped", bufs=2))
+        code_pool = ctx.enter_context(tc.tile_pool(name="codes", bufs=HEADS))
+        a_pool = ctx.enter_context(tc.tile_pool(name="a", bufs=2))
+        g_pool = ctx.enter_context(tc.tile_pool(name="g", bufs=ROUND_UNITS + 1))
+        root_pool = ctx.enter_context(tc.tile_pool(name="root", bufs=ROUND_UNITS))
+        result_pool = ctx.enter_context(tc.tile_pool(name="result", bufs=ROW_TILES * ROUND_UNITS + 3))
+        fresh_pool = ctx.enter_context(tc.tile_pool(name="fresh", bufs=3))
         sum_pool = ctx.enter_context(tc.psum_pool(name="sums", bufs=4))
         turn_pool = ctx.enter_context(tc.psum_pool(name="turned", bufs=4))
         ctx.enter_context(tc.manual_schedule())
@@ -51,6 +57,7 @@ def tile_rglru_t_e_kernel(
         x_of, state_of = {}, {}
         grouped_of, codes_of, planes_of = {}, {}, {}
         a_of, g_of, root_of = {}, {}, {}
+        result_of = {}
 
         def load_x(b):
             x_sb = x_pool.tile([P, ROW_TILES, CHANNELS], BF16)
@@ -109,9 +116,10 @@ def tile_rglru_t_e_kernel(
         nc.scalar.activation(out=soft[:], in_=soft[:], func=ACT.Exp, scale=-1.0)
         nc.scalar.activation(out=soft[:], in_=soft[:], func=ACT.Ln, bias=one[:])
 
-        def regroup(b, h):
+        def regroup(u):
+            b, h = divmod(u, HEADS)
             x_words = x_of[b][:].bitcast(F32)
-            grouped = quant_pool.tile([P, BLOCK, PACK], BF16, align_bytes=64)
+            grouped = grouped_pool.tile([P, BLOCK, PACK], BF16, align_bytes=64)
             grouped_words = grouped[:].bitcast(F32)
             for pair in range(ROW_TILES // 2):
                 turned = turn_pool.tile([P, 2, 2, P], F32, tag="turned")
@@ -128,25 +136,26 @@ def tile_rglru_t_e_kernel(
                     ),
                     in_=turned[:].rearrange("p i w r -> p i r w"),
                 )
-            grouped_of[b, h] = grouped
+            grouped_of[u] = grouped
 
-        def quantise(b, h):
-            codes = quant_pool.tile([P, BLOCK], U32, align_bytes=64)
-            plane = quant_pool.tile([P, BLOCK], U8, align_bytes=64)
+        def quantise(u):
+            codes = code_pool.tile([P, BLOCK], U32, align_bytes=64)
+            plane = code_pool.tile([P, BLOCK], U8, align_bytes=64)
             nc.vector.quantize_mx(
                 out=codes[:].bitcast(FP8X4),
                 scales=plane[:],
-                in_=grouped_of[b, h][:].rearrange("p r t -> p (r t)"),
+                in_=grouped_of[u][:].rearrange("p r t -> p (r t)"),
             )
-            codes_of[b, h], planes_of[b, h] = codes, plane
+            codes_of[u], planes_of[u] = codes, plane
 
-        def open_unit(b, h):
-            a_t = gate_pool.tile([P, CHANNEL_TILES, BLOCK], F32)
-            g_t = gate_pool.tile([P, CHANNEL_TILES, BLOCK], F32)
+        def open_unit(u):
+            a_t = a_pool.tile([P, CHANNEL_TILES, BLOCK], F32)
+            g_t = g_pool.tile([P, CHANNEL_TILES, BLOCK], F32)
             root_t = root_pool.tile([P, CHANNEL_TILES, BLOCK], F32)
-            a_of[b, h], g_of[b, h], root_of[b, h] = a_t, g_t, root_t
+            a_of[u], g_of[u], root_of[u] = a_t, g_t, root_t
 
-        def gates(b, h, m):
+        def gates(u, m):
+            h = u % HEADS
             channels = slice(P * m, P * (m + 1))
             column = CHANNEL_TILES * h + m
             sums = {}
@@ -156,14 +165,14 @@ def tile_rglru_t_e_kernel(
                     out=acc[:],
                     lhsT=w_codes[:, HEADS * gate + h, channels].bitcast(FP8X4),
                     lhsT_scale=w_planes[:, HEADS * gate + h, channels],
-                    rhs=codes_of[b, h][:].bitcast(FP8X4),
-                    rhs_scale=planes_of[b, h][:],
+                    rhs=codes_of[u][:].bitcast(FP8X4),
+                    rhs_scale=planes_of[u][:],
                     start=True,
                     stop=True,
                 )
                 sums[gate] = acc
-            a_part = a_of[b, h][:, m, :]
-            for gate, target in ((GATE_A, a_part), (GATE_X, g_of[b, h][:, m, :])):
+            a_part = a_of[u][:, m, :]
+            for gate, target in ((GATE_A, a_part), (GATE_X, g_of[u][:, m, :])):
                 nc.scalar.activation(
                     out=target,
                     in_=sums[gate][:],
@@ -178,12 +187,12 @@ def tile_rglru_t_e_kernel(
                 bias=minus_4c[:, column : column + 1],
                 scale=minus_4c[:, column : column + 1],
             )
-            nc.gpsimd.tensor_tensor(out=root_of[b, h][:, m, :], in0=a_part, in1=a_part, op=ALU.mult)
+            nc.gpsimd.tensor_tensor(out=root_of[u][:, m, :], in0=a_part, in1=a_part, op=ALU.mult)
 
-        def roots(b, h):
+        def roots(u):
             for first in range(0, CHANNEL_TILES, ROOT_TILES):
-                root_part = root_of[b, h][:, first : first + ROOT_TILES, :]
-                g_part = g_of[b, h][:, first : first + ROOT_TILES, :]
+                root_part = root_of[u][:, first : first + ROOT_TILES, :]
+                g_part = g_of[u][:, first : first + ROOT_TILES, :]
                 nc.scalar.activation(
                     out=root_part, in_=root_part, func=ACT.Sqrt, bias=quarter[:], scale=-0.25
                 )
@@ -191,54 +200,70 @@ def tile_rglru_t_e_kernel(
                     out=g_part, in0=g_part, scalar=1.0, in1=root_part, op0=ALU.add, op1=ALU.mult
                 )
 
-        def combine(b, h, t):
-            rows = slice(P * t, P * (t + 1))
-            channels = slice(HEAD * h, HEAD * (h + 1))
-            turned_of = {}
-            for factor, source in (("a", a_of[b, h]), ("g", g_of[b, h])):
-                turned = turn_pool.tile([P, HEAD], F32, tag="turned")
-                for m in range(CHANNEL_TILES):
-                    nc.tensor.transpose(turned[:, P * m : P * (m + 1)], source[:, m, rows], ident[:])
-                turned_of[factor] = turned
-            result = out_pool.tile([P, HEAD], F32)
+        def turn_back(source, rows):
+            turned = turn_pool.tile([P, HEAD], F32, tag="turned")
+            for m in range(CHANNEL_TILES):
+                nc.tensor.transpose(turned[:, P * m : P * (m + 1)], source[:, m, rows], ident[:])
+            return turned
+
+        def keep_state(u, t):
+            b, h = divmod(u, HEADS)
+            a_rows = turn_back(a_of[u], slice(P * t, P * (t + 1)))
+            result = result_pool.tile([P, HEAD], F32)
             nc.vector.tensor_tensor(
-                out=result[:], in0=turned_of["a"][:], in1=state_of[b][:, t, channels], op=ALU.mult
+                out=result[:],
+                in0=a_rows[:],
+                in1=state_of[b][:, t, HEAD * h : HEAD * (h + 1)],
+                op=ALU.mult,
             )
-            fresh = out_pool.tile([P, HEAD], F32)
+            result_of[u, t] = result
+
+        def finish(u, t):
+            b, h = divmod(u, HEADS)
+            channels = slice(HEAD * h, HEAD * (h + 1))
+            g_rows = turn_back(g_of[u], slice(P * t, P * (t + 1)))
+            fresh = fresh_pool.tile([P, HEAD], F32)
             nc.vector.tensor_tensor(
-                out=fresh[:], in0=turned_of["g"][:], in1=x_of[b][:, t, channels], op=ALU.mult
+                out=fresh[:], in0=g_rows[:], in1=x_of[b][:, t, channels], op=ALU.mult
             )
             adder = nc.gpsimd if h == 0 else nc.vector
+            result = result_of[u, t]
             adder.tensor_tensor(out=result[:], in0=result[:], in1=fresh[:], op=ALU.add)
             nc.sync.dma_start(out=out_blocks[b][:, t, channels], in_=result[:])
 
-        for h in range(HEADS):
-            regroup(0, h)
-            quantise(0, h)
+        for u in range(HEADS):
+            regroup(u)
+            quantise(u)
         nc.vector.scalar_tensor_tensor(
             out=soft[:], in0=a_par[:], scalar=0.0, in1=soft[:], op0=ALU.max, op1=ALU.add
         )
         minus_4c = keep.tile([P, 8], F32)
         nc.vector.tensor_scalar_mul(out=minus_4c[:], in0=soft[:], scalar1=-4.0)
+        load_state(0)
+        for b in range(1, X_BLOCKS):
+            load_x(b)
+        load_state(1)
 
-        for b in range(BLOCKS + 1):
-            if b + 1 < BLOCKS:
-                load_x(b + 1)
-            if b < BLOCKS:
-                load_state(b)
-            for h in range(HEADS):
-                if b < BLOCKS:
-                    open_unit(b, h)
-                for step in range(CHANNEL_TILES):
-                    if b < BLOCKS:
-                        gates(b, h, step)
-                    if b >= 1:
-                        combine(b - 1, h, step)
-            if b + 1 < BLOCKS:
-                for h in range(HEADS):
-                    regroup(b + 1, h)
-                for h in range(HEADS):
-                    quantise(b + 1, h)
-            if b < BLOCKS:
-                for h in range(HEADS):
-                    roots(b, h)
+        for i in range(UNITS + ROUND_UNITS):
+            kept, done = i - 1, i - ROUND_UNITS
+            if i < UNITS:
+                open_unit(i)
+            for step in range(CHANNEL_TILES):
+                if i < UNITS:
+                    gates(i, step)
+                if 0 <= kept < UNITS:
+                    keep_state(kept, step)
+                if done >= 0:
+                    finish(done, step)
+            if kept >= 0 and kept % HEADS == HEADS - 1 and kept // HEADS + 2 < BLOCKS:
+                load_state(kept // HEADS + 2)
+            if done >= 0 and done % HEADS == HEADS - 1 and done // HEADS + X_BLOCKS < BLOCKS:
+                load_x(done // HEADS + X_BLOCKS)
+            if i % HEADS == HEADS - 1 and i + HEADS < UNITS:
+                for u in range(i + 1, i + 1 + HEADS):
+                    regroup(u)
+                for u in range(i + 1, i + 1 + HEADS):
+                    quantise(u)
+            if i % ROUND_UNITS == ROUND_UNITS - 1 and i < UNITS:
+                for u in range(i + 1 - ROUND_UNITS, i + 1):
+                    roots(u)

@@ -25,7 +25,7 @@ CHANNEL_TILES = HEAD // P
 GATE_X, GATE_A = 0, 1
 ROOT_TILES = 2
 UNITS = BLOCKS * HEADS
-ROUND_UNITS = 4
+ROUND_UNITS = 2
 X_BLOCKS = ROUND_UNITS // HEADS + 2
 
 FLOPS = 2 * ROWS * HEAD * HEAD * HEADS * 2
@@ -45,11 +45,11 @@ def tile_rglru_t_e_kernel(
         state_pool = ctx.enter_context(tc.tile_pool(name="state", bufs=2))
         grouped_pool = ctx.enter_context(tc.tile_pool(name="grouped", bufs=2))
         code_pool = ctx.enter_context(tc.tile_pool(name="codes", bufs=HEADS))
-        a_pool = ctx.enter_context(tc.tile_pool(name="a", bufs=2))
+        a_pool = ctx.enter_context(tc.tile_pool(name="a", bufs=3))
         g_pool = ctx.enter_context(tc.tile_pool(name="g", bufs=ROUND_UNITS + 1))
         root_pool = ctx.enter_context(tc.tile_pool(name="root", bufs=ROUND_UNITS))
-        result_pool = ctx.enter_context(tc.tile_pool(name="result", bufs=ROW_TILES * ROUND_UNITS + 3))
-        fresh_pool = ctx.enter_context(tc.tile_pool(name="fresh", bufs=3))
+        result_pool = ctx.enter_context(tc.tile_pool(name="result", bufs=ROW_TILES * (ROUND_UNITS + 1)))
+        fresh_pool = ctx.enter_context(tc.tile_pool(name="fresh", bufs=ROW_TILES))
         sum_pool = ctx.enter_context(tc.psum_pool(name="sums", bufs=4))
         turn_pool = ctx.enter_context(tc.psum_pool(name="turned", bufs=4))
         ctx.enter_context(tc.manual_schedule())
@@ -187,7 +187,11 @@ def tile_rglru_t_e_kernel(
                 bias=minus_4c[:, column : column + 1],
                 scale=minus_4c[:, column : column + 1],
             )
-            nc.gpsimd.tensor_tensor(out=root_of[u][:, m, :], in0=a_part, in1=a_part, op=ALU.mult)
+
+        def square(u, m):
+            squarer = nc.gpsimd if u % HEADS == 0 else nc.vector
+            a_part = a_of[u][:, m, :]
+            squarer.tensor_tensor(out=root_of[u][:, m, :], in0=a_part, in1=a_part, op=ALU.mult)
 
         def roots(u):
             for first in range(0, CHANNEL_TILES, ROOT_TILES):
@@ -226,9 +230,8 @@ def tile_rglru_t_e_kernel(
             nc.vector.tensor_tensor(
                 out=fresh[:], in0=g_rows[:], in1=x_of[b][:, t, channels], op=ALU.mult
             )
-            adder = nc.gpsimd if h == 0 else nc.vector
             result = result_of[u, t]
-            adder.tensor_tensor(out=result[:], in0=result[:], in1=fresh[:], op=ALU.add)
+            nc.gpsimd.tensor_tensor(out=result[:], in0=result[:], in1=fresh[:], op=ALU.add)
             nc.sync.dma_start(out=out_blocks[b][:, t, channels], in_=result[:])
 
         for u in range(HEADS):
@@ -255,6 +258,8 @@ def tile_rglru_t_e_kernel(
                     keep_state(kept, step)
                 if done >= 0:
                     finish(done, step)
+                if i < UNITS:
+                    square(i, step)
             if kept >= 0 and kept % HEADS == HEADS - 1 and kept // HEADS + 2 < BLOCKS:
                 load_state(kept // HEADS + 2)
             if done >= 0 and done % HEADS == HEADS - 1 and done // HEADS + X_BLOCKS < BLOCKS:

@@ -46,10 +46,10 @@ def tile_rglru_t_e_kernel(
         grouped_pool = ctx.enter_context(tc.tile_pool(name="grouped", bufs=2))
         code_pool = ctx.enter_context(tc.tile_pool(name="codes", bufs=HEADS))
         a_pool = ctx.enter_context(tc.tile_pool(name="a", bufs=3))
-        g_pool = ctx.enter_context(tc.tile_pool(name="g", bufs=ROUND_UNITS + 1))
-        root_pool = ctx.enter_context(tc.tile_pool(name="root", bufs=ROUND_UNITS))
+        g_pool = ctx.enter_context(tc.tile_pool(name="g", bufs=3))
+        root_pool = ctx.enter_context(tc.tile_pool(name="root", bufs=ROUND_UNITS + 2))
         result_pool = ctx.enter_context(tc.tile_pool(name="result", bufs=ROW_TILES * (ROUND_UNITS + 1)))
-        fresh_pool = ctx.enter_context(tc.tile_pool(name="fresh", bufs=ROW_TILES))
+        fresh_pool = ctx.enter_context(tc.tile_pool(name="fresh", bufs=ROW_TILES * (ROUND_UNITS + 1)))
         sum_pool = ctx.enter_context(tc.psum_pool(name="sums", bufs=4))
         turn_pool = ctx.enter_context(tc.psum_pool(name="turned", bufs=4))
         ctx.enter_context(tc.manual_schedule())
@@ -57,7 +57,7 @@ def tile_rglru_t_e_kernel(
         x_of, state_of = {}, {}
         grouped_of, codes_of, planes_of = {}, {}, {}
         a_of, g_of, root_of = {}, {}, {}
-        result_of = {}
+        result_of, fresh_of = {}, {}
 
         def load_x(b):
             x_sb = x_pool.tile([P, ROW_TILES, CHANNELS], BF16)
@@ -189,19 +189,14 @@ def tile_rglru_t_e_kernel(
             )
 
         def square(u, m):
-            squarer = nc.gpsimd if u % HEADS == 0 else nc.vector
             a_part = a_of[u][:, m, :]
-            squarer.tensor_tensor(out=root_of[u][:, m, :], in0=a_part, in1=a_part, op=ALU.mult)
+            nc.gpsimd.tensor_tensor(out=root_of[u][:, m, :], in0=a_part, in1=a_part, op=ALU.mult)
 
         def roots(u):
             for first in range(0, CHANNEL_TILES, ROOT_TILES):
                 root_part = root_of[u][:, first : first + ROOT_TILES, :]
-                g_part = g_of[u][:, first : first + ROOT_TILES, :]
                 nc.scalar.activation(
                     out=root_part, in_=root_part, func=ACT.Sqrt, bias=quarter[:], scale=-0.25
-                )
-                nc.vector.scalar_tensor_tensor(
-                    out=g_part, in0=g_part, scalar=1.0, in1=root_part, op0=ALU.add, op1=ALU.mult
                 )
 
         def turn_back(source, rows):
@@ -221,15 +216,24 @@ def tile_rglru_t_e_kernel(
                 op=ALU.mult,
             )
             result_of[u, t] = result
+            tanh_rows = turn_back(g_of[u], slice(P * t, P * (t + 1)))
+            fresh = fresh_pool.tile([P, HEAD], F32)
+            nc.vector.scalar_tensor_tensor(
+                out=fresh[:],
+                in0=tanh_rows[:],
+                scalar=1.0,
+                in1=x_of[b][:, t, HEAD * h : HEAD * (h + 1)],
+                op0=ALU.add,
+                op1=ALU.mult,
+            )
+            fresh_of[u, t] = fresh
 
         def finish(u, t):
             b, h = divmod(u, HEADS)
             channels = slice(HEAD * h, HEAD * (h + 1))
-            g_rows = turn_back(g_of[u], slice(P * t, P * (t + 1)))
-            fresh = fresh_pool.tile([P, HEAD], F32)
-            nc.vector.tensor_tensor(
-                out=fresh[:], in0=g_rows[:], in1=x_of[b][:, t, channels], op=ALU.mult
-            )
+            root_rows = turn_back(root_of[u], slice(P * t, P * (t + 1)))
+            fresh = fresh_of[u, t]
+            nc.vector.tensor_tensor(out=fresh[:], in0=root_rows[:], in1=fresh[:], op=ALU.mult)
             result = result_of[u, t]
             nc.gpsimd.tensor_tensor(out=result[:], in0=result[:], in1=fresh[:], op=ALU.add)
             nc.sync.dma_start(out=out_blocks[b][:, t, channels], in_=result[:])
@@ -262,8 +266,8 @@ def tile_rglru_t_e_kernel(
                     square(i, step)
             if kept >= 0 and kept % HEADS == HEADS - 1 and kept // HEADS + 2 < BLOCKS:
                 load_state(kept // HEADS + 2)
-            if done >= 0 and done % HEADS == HEADS - 1 and done // HEADS + X_BLOCKS < BLOCKS:
-                load_x(done // HEADS + X_BLOCKS)
+            if kept >= 0 and kept % HEADS == HEADS - 1 and kept // HEADS + X_BLOCKS < BLOCKS:
+                load_x(kept // HEADS + X_BLOCKS)
             if i % HEADS == HEADS - 1 and i + HEADS < UNITS:
                 for u in range(i + 1, i + 1 + HEADS):
                     regroup(u)

@@ -25,8 +25,11 @@ CHANNEL_TILES = HEAD // P
 GATE_X, GATE_A = 0, 1
 ROOT_TILES = 2
 UNITS = BLOCKS * HEADS
-ROUND_UNITS = 2
-X_BLOCKS = ROUND_UNITS // HEADS + 2
+STEPS = UNITS * CHANNEL_TILES
+ROUND_UNITS = 4
+X_BLOCKS = 3
+A_TILES = 10
+STORE_STEP = 2
 
 FLOPS = 2 * ROWS * HEAD * HEAD * HEADS * 2
 
@@ -44,20 +47,20 @@ def tile_rglru_t_e_kernel(
         x_pool = ctx.enter_context(tc.tile_pool(name="x", bufs=X_BLOCKS))
         state_pool = ctx.enter_context(tc.tile_pool(name="state", bufs=2))
         grouped_pool = ctx.enter_context(tc.tile_pool(name="grouped", bufs=2))
-        code_pool = ctx.enter_context(tc.tile_pool(name="codes", bufs=HEADS))
-        a_pool = ctx.enter_context(tc.tile_pool(name="a", bufs=3))
-        g_pool = ctx.enter_context(tc.tile_pool(name="g", bufs=3))
-        root_pool = ctx.enter_context(tc.tile_pool(name="root", bufs=ROUND_UNITS + 2))
-        result_pool = ctx.enter_context(tc.tile_pool(name="result", bufs=ROW_TILES * (ROUND_UNITS + 1)))
-        fresh_pool = ctx.enter_context(tc.tile_pool(name="fresh", bufs=ROW_TILES * (ROUND_UNITS + 1)))
+        code_pool = ctx.enter_context(tc.tile_pool(name="codes", bufs=2))
+        a_pool = ctx.enter_context(tc.tile_pool(name="a", bufs=A_TILES))
+        tanh_pool = ctx.enter_context(tc.tile_pool(name="tanh", bufs=4))
+        root_pool = ctx.enter_context(tc.tile_pool(name="root", bufs=ROUND_UNITS))
+        result_pool = ctx.enter_context(tc.tile_pool(name="result", bufs=ROUND_UNITS + 1))
+        fresh_pool = ctx.enter_context(tc.tile_pool(name="fresh", bufs=ROUND_UNITS + 1))
         sum_pool = ctx.enter_context(tc.psum_pool(name="sums", bufs=4))
         turn_pool = ctx.enter_context(tc.psum_pool(name="turned", bufs=4))
         ctx.enter_context(tc.manual_schedule())
 
         x_of, state_of = {}, {}
         grouped_of, codes_of, planes_of = {}, {}, {}
-        a_of, g_of, root_of = {}, {}, {}
-        result_of, fresh_of = {}, {}
+        sums_of, a_of, tanh_of = {}, {}, {}
+        root_of, result_of, fresh_of = {}, {}, {}
 
         def load_x(b):
             x_sb = x_pool.tile([P, ROW_TILES, CHANNELS], BF16)
@@ -116,81 +119,120 @@ def tile_rglru_t_e_kernel(
         nc.scalar.activation(out=soft[:], in_=soft[:], func=ACT.Exp, scale=-1.0)
         nc.scalar.activation(out=soft[:], in_=soft[:], func=ACT.Ln, bias=one[:])
 
-        def regroup(u):
-            b, h = divmod(u, HEADS)
+        def regroup(b, piece):
+            h, pair = divmod(piece, ROW_TILES // 2)
+            if piece == 0:
+                grouped = grouped_pool.tile([P, HEADS, BLOCK, PACK], BF16, align_bytes=64)
+                grouped_of[b] = grouped
             x_words = x_of[b][:].bitcast(F32)
-            grouped = grouped_pool.tile([P, BLOCK, PACK], BF16, align_bytes=64)
-            grouped_words = grouped[:].bitcast(F32)
-            for pair in range(ROW_TILES // 2):
-                turned = turn_pool.tile([P, 2, 2, P], F32, tag="turned")
-                for i in range(2):
-                    for w in range(2):
-                        nc.tensor.transpose(
-                            turned[:, i, w, :],
-                            x_words[:, 2 * pair + i, 256 * h + w : 256 * (h + 1) : 2],
-                            ident[:],
-                        )
-                nc.vector.tensor_copy(
-                    out=grouped_words[:, 2 * P * pair : 2 * P * (pair + 1), :].rearrange(
-                        "p (i r) w -> p i r w", i=2
-                    ),
-                    in_=turned[:].rearrange("p i w r -> p i r w"),
-                )
-            grouped_of[u] = grouped
-
-        def quantise(u):
-            codes = code_pool.tile([P, BLOCK], U32, align_bytes=64)
-            plane = code_pool.tile([P, BLOCK], U8, align_bytes=64)
-            nc.vector.quantize_mx(
-                out=codes[:].bitcast(FP8X4),
-                scales=plane[:],
-                in_=grouped_of[u][:].rearrange("p r t -> p (r t)"),
+            grouped_words = grouped_of[b][:].bitcast(F32)
+            turned = turn_pool.tile([P, 2, 2, P], F32, tag="turned")
+            for i in range(2):
+                for w in range(2):
+                    nc.tensor.transpose(
+                        turned[:, i, w, :],
+                        x_words[:, 2 * pair + i, 256 * h + w : 256 * (h + 1) : 2],
+                        ident[:],
+                    )
+            nc.vector.tensor_copy(
+                out=grouped_words[:, h, 2 * P * pair : 2 * P * (pair + 1), :].rearrange(
+                    "p (i r) w -> p i r w", i=2
+                ),
+                in_=turned[:].rearrange("p i w r -> p i r w"),
             )
-            codes_of[u], planes_of[u] = codes, plane
+
+        def open_codes(b):
+            codes = code_pool.tile([P, HEADS * BLOCK], U32, align_bytes=64)
+            plane = code_pool.tile([P, HEADS * BLOCK], U8, align_bytes=64)
+            codes_of[b], planes_of[b] = codes, plane
+
+        def quantise(b, first, heads):
+            columns = slice(BLOCK * first, BLOCK * (first + heads))
+            nc.vector.quantize_mx(
+                out=codes_of[b][:, columns].bitcast(FP8X4),
+                scales=planes_of[b][:, columns],
+                in_=grouped_of[b][:, first : first + heads, :, :].rearrange("p h r t -> p (h r t)"),
+            )
 
         def open_unit(u):
-            a_t = a_pool.tile([P, CHANNEL_TILES, BLOCK], F32)
-            g_t = g_pool.tile([P, CHANNEL_TILES, BLOCK], F32)
             root_t = root_pool.tile([P, CHANNEL_TILES, BLOCK], F32)
-            a_of[u], g_of[u], root_of[u] = a_t, g_t, root_t
+            result = result_pool.tile([P, ROW_TILES, HEAD], F32)
+            fresh = fresh_pool.tile([P, ROW_TILES, HEAD], F32)
+            root_of[u], result_of[u], fresh_of[u] = root_t, result, fresh
 
-        def gates(u, m):
-            h = u % HEADS
+        def passes(s):
+            u, m = divmod(s, CHANNEL_TILES)
+            b, h = divmod(u, HEADS)
             channels = slice(P * m, P * (m + 1))
-            column = CHANNEL_TILES * h + m
-            sums = {}
+            rows = slice(BLOCK * h, BLOCK * (h + 1))
             for gate in (GATE_A, GATE_X):
                 acc = sum_pool.tile([P, BLOCK], F32)
                 nc.tensor.matmul_mx(
                     out=acc[:],
                     lhsT=w_codes[:, HEADS * gate + h, channels].bitcast(FP8X4),
                     lhsT_scale=w_planes[:, HEADS * gate + h, channels],
-                    rhs=codes_of[u][:].bitcast(FP8X4),
-                    rhs_scale=planes_of[u][:],
+                    rhs=codes_of[b][:, rows].bitcast(FP8X4),
+                    rhs_scale=planes_of[b][:, rows],
                     start=True,
                     stop=True,
                 )
-                sums[gate] = acc
-            a_part = a_of[u][:, m, :]
-            for gate, target in ((GATE_A, a_part), (GATE_X, g_of[u][:, m, :])):
+                sums_of[s, gate] = acc
+
+        def gates(s):
+            u, m = divmod(s, CHANNEL_TILES)
+            column = CHANNEL_TILES * (u % HEADS) + m
+            a_t = a_pool.tile([P, BLOCK], F32)
+            tanh_t = tanh_pool.tile([P, BLOCK], F32)
+            for gate, target in ((GATE_A, a_t), (GATE_X, tanh_t)):
                 nc.scalar.activation(
-                    out=target,
-                    in_=sums[gate][:],
+                    out=target[:],
+                    in_=sums_of[s, gate][:],
                     func=ACT.Tanh,
                     bias=half_bias[:, 8 * gate + column : 8 * gate + column + 1],
                     scale=0.5,
                 )
             nc.scalar.activation(
-                out=a_part,
-                in_=a_part,
+                out=a_t[:],
+                in_=a_t[:],
                 func=ACT.Exp,
                 bias=minus_4c[:, column : column + 1],
                 scale=minus_4c[:, column : column + 1],
             )
+            a_of[s], tanh_of[s] = a_t, tanh_t
 
-        def square(u, m):
-            a_part = a_of[u][:, m, :]
-            nc.gpsimd.tensor_tensor(out=root_of[u][:, m, :], in0=a_part, in1=a_part, op=ALU.mult)
+        def square(s):
+            u, m = divmod(s, CHANNEL_TILES)
+            nc.gpsimd.tensor_tensor(
+                out=root_of[u][:, m, :], in0=a_of[s][:], in1=a_of[s][:], op=ALU.mult
+            )
+
+        def turn_back(source):
+            turned = turn_pool.tile([P, ROW_TILES, P], F32, tag="turned")
+            for t in range(ROW_TILES):
+                nc.tensor.transpose(turned[:, t, :], source[:, P * t : P * (t + 1)], ident[:])
+            return turned
+
+        def keep_granule(s):
+            u, m = divmod(s, CHANNEL_TILES)
+            b, h = divmod(u, HEADS)
+            inside = slice(P * m, P * (m + 1))
+            channels = slice(HEAD * h + P * m, HEAD * h + P * (m + 1))
+            a_rows = turn_back(a_of[s])
+            nc.vector.tensor_tensor(
+                out=result_of[u][:, :, inside],
+                in0=a_rows[:],
+                in1=state_of[b][:, :, channels],
+                op=ALU.mult,
+            )
+            tanh_rows = turn_back(tanh_of[s])
+            nc.vector.scalar_tensor_tensor(
+                out=fresh_of[u][:, :, inside],
+                in0=tanh_rows[:],
+                scalar=1.0,
+                in1=x_of[b][:, :, channels],
+                op0=ALU.add,
+                op1=ALU.mult,
+            )
 
         def roots(u):
             for first in range(0, CHANNEL_TILES, ROOT_TILES):
@@ -199,48 +241,25 @@ def tile_rglru_t_e_kernel(
                     out=root_part, in_=root_part, func=ACT.Sqrt, bias=quarter[:], scale=-0.25
                 )
 
-        def turn_back(source, rows):
-            turned = turn_pool.tile([P, HEAD], F32, tag="turned")
-            for m in range(CHANNEL_TILES):
-                nc.tensor.transpose(turned[:, P * m : P * (m + 1)], source[:, m, rows], ident[:])
-            return turned
+        def finish(u, m, adder):
+            inside = slice(P * m, P * (m + 1))
+            root_rows = turn_back(root_of[u][:, m, :])
+            fresh_part = fresh_of[u][:, :, inside]
+            result_part = result_of[u][:, :, inside]
+            nc.vector.tensor_tensor(out=fresh_part, in0=root_rows[:], in1=fresh_part, op=ALU.mult)
+            adder.tensor_tensor(out=result_part, in0=result_part, in1=fresh_part, op=ALU.add)
 
-        def keep_state(u, t):
+        def store(u):
             b, h = divmod(u, HEADS)
-            a_rows = turn_back(a_of[u], slice(P * t, P * (t + 1)))
-            result = result_pool.tile([P, HEAD], F32)
-            nc.vector.tensor_tensor(
-                out=result[:],
-                in0=a_rows[:],
-                in1=state_of[b][:, t, HEAD * h : HEAD * (h + 1)],
-                op=ALU.mult,
+            nc.sync.dma_start(
+                out=out_blocks[b][:, :, HEAD * h : HEAD * (h + 1)], in_=result_of[u][:]
             )
-            result_of[u, t] = result
-            tanh_rows = turn_back(g_of[u], slice(P * t, P * (t + 1)))
-            fresh = fresh_pool.tile([P, HEAD], F32)
-            nc.vector.scalar_tensor_tensor(
-                out=fresh[:],
-                in0=tanh_rows[:],
-                scalar=1.0,
-                in1=x_of[b][:, t, HEAD * h : HEAD * (h + 1)],
-                op0=ALU.add,
-                op1=ALU.mult,
-            )
-            fresh_of[u, t] = fresh
 
-        def finish(u, t):
-            b, h = divmod(u, HEADS)
-            channels = slice(HEAD * h, HEAD * (h + 1))
-            root_rows = turn_back(root_of[u], slice(P * t, P * (t + 1)))
-            fresh = fresh_of[u, t]
-            nc.vector.tensor_tensor(out=fresh[:], in0=root_rows[:], in1=fresh[:], op=ALU.mult)
-            result = result_of[u, t]
-            nc.gpsimd.tensor_tensor(out=result[:], in0=result[:], in1=fresh[:], op=ALU.add)
-            nc.sync.dma_start(out=out_blocks[b][:, t, channels], in_=result[:])
-
-        for u in range(HEADS):
-            regroup(u)
-            quantise(u)
+        open_codes(0)
+        for h in range(HEADS):
+            for pair in range(ROW_TILES // 2):
+                regroup(0, (ROW_TILES // 2) * h + pair)
+            quantise(0, h, 1)
         nc.vector.scalar_tensor_tensor(
             out=soft[:], in0=a_par[:], scalar=0.0, in1=soft[:], op0=ALU.max, op1=ALU.add
         )
@@ -251,28 +270,54 @@ def tile_rglru_t_e_kernel(
             load_x(b)
         load_state(1)
 
-        for i in range(UNITS + ROUND_UNITS):
-            kept, done = i - 1, i - ROUND_UNITS
-            if i < UNITS:
-                open_unit(i)
-            for step in range(CHANNEL_TILES):
-                if i < UNITS:
-                    gates(i, step)
-                if 0 <= kept < UNITS:
-                    keep_state(kept, step)
-                if done >= 0:
-                    finish(done, step)
-                if i < UNITS:
-                    square(i, step)
-            if kept >= 0 and kept % HEADS == HEADS - 1 and kept // HEADS + 2 < BLOCKS:
-                load_state(kept // HEADS + 2)
-            if kept >= 0 and kept % HEADS == HEADS - 1 and kept // HEADS + X_BLOCKS < BLOCKS:
-                load_x(kept // HEADS + X_BLOCKS)
-            if i % HEADS == HEADS - 1 and i + HEADS < UNITS:
-                for u in range(i + 1, i + 1 + HEADS):
-                    regroup(u)
-                for u in range(i + 1, i + 1 + HEADS):
-                    quantise(u)
-            if i % ROUND_UNITS == ROUND_UNITS - 1 and i < UNITS:
-                for u in range(i + 1 - ROUND_UNITS, i + 1):
-                    roots(u)
+        done = {"passes": 0, "keep": 0, "store": 0}
+
+        def passes_up_to(last):
+            for s in range(done["passes"], min(last, STEPS - 1) + 1):
+                passes(s)
+                done["passes"] = s + 1
+
+        def keep_up_to(last):
+            for s in range(done["keep"], last + 1):
+                keep_granule(s)
+                done["keep"] = s + 1
+
+        finished = []
+        for s in range(STEPS):
+            u, m = divmod(s, CHANNEL_TILES)
+            b, h = divmod(u, HEADS)
+            if m == 0:
+                open_unit(u)
+            passes_up_to(s + 1)
+            gates(s)
+            keep_up_to(s - 1)
+            if h == 0 and b + 1 < BLOCKS:
+                regroup(b + 1, m)
+            if h == 1 and m == 1 and b + 1 < BLOCKS:
+                open_codes(b + 1)
+                quantise(b + 1, 0, HEADS)
+            if h == 0 and m == 0 and b >= 1:
+                if b + X_BLOCKS - 1 < BLOCKS:
+                    load_x(b + X_BLOCKS - 1)
+                if b + 1 < BLOCKS:
+                    load_state(b + 1)
+            if m == STORE_STEP and done["store"] < len(finished):
+                store(finished[done["store"]])
+                done["store"] += 1
+            square(s)
+            if u % ROUND_UNITS == ROUND_UNITS - 1 and m == CHANNEL_TILES - 1:
+                last_round = u == UNITS - 1
+                passes_up_to(s + 2)
+                keep_up_to(s)
+                members = range(u + 1 - ROUND_UNITS, u + 1)
+                for v in members:
+                    roots(v)
+                for v in members:
+                    for mm in range(CHANNEL_TILES):
+                        helper = last_round and mm % 2 == 1
+                        finish(v, mm, nc.vector if helper else nc.gpsimd)
+                    finished.append(v)
+                    if last_round:
+                        for w in finished[done["store"] :]:
+                            store(w)
+                        done["store"] = len(finished)

@@ -28,7 +28,7 @@ UNITS = BLOCKS * HEADS
 STEPS = UNITS * CHANNEL_TILES
 ROUND_UNITS = 4
 X_BLOCKS = 3
-A_TILES = 10
+A_UNITS = 4
 STORE_STEP = 2
 
 FLOPS = 2 * ROWS * HEAD * HEAD * HEADS * 2
@@ -48,7 +48,7 @@ def tile_rglru_t_e_kernel(
         state_pool = ctx.enter_context(tc.tile_pool(name="state", bufs=2))
         grouped_pool = ctx.enter_context(tc.tile_pool(name="grouped", bufs=2))
         code_pool = ctx.enter_context(tc.tile_pool(name="codes", bufs=2))
-        a_pool = ctx.enter_context(tc.tile_pool(name="a", bufs=A_TILES))
+        a_pool = ctx.enter_context(tc.tile_pool(name="a", bufs=A_UNITS))
         tanh_pool = ctx.enter_context(tc.tile_pool(name="tanh", bufs=4))
         root_pool = ctx.enter_context(tc.tile_pool(name="root", bufs=ROUND_UNITS))
         result_pool = ctx.enter_context(tc.tile_pool(name="result", bufs=ROUND_UNITS + 1))
@@ -59,8 +59,8 @@ def tile_rglru_t_e_kernel(
 
         x_of, state_of = {}, {}
         grouped_of, codes_of, planes_of = {}, {}, {}
-        sums_of, a_of, tanh_of = {}, {}, {}
-        root_of, result_of, fresh_of = {}, {}, {}
+        sums_of, tanh_of = {}, {}
+        a_of, root_of, result_of, fresh_of = {}, {}, {}, {}
 
         def load_x(b):
             x_sb = x_pool.tile([P, ROW_TILES, CHANNELS], BF16)
@@ -155,6 +155,8 @@ def tile_rglru_t_e_kernel(
             )
 
         def open_unit(u):
+            a_t = a_pool.tile([P, CHANNEL_TILES, BLOCK], F32)
+            a_of[u] = a_t
             root_t = root_pool.tile([P, CHANNEL_TILES, BLOCK], F32)
             result = result_pool.tile([P, ROW_TILES, HEAD], F32)
             fresh = fresh_pool.tile([P, ROW_TILES, HEAD], F32)
@@ -181,30 +183,27 @@ def tile_rglru_t_e_kernel(
         def gates(s):
             u, m = divmod(s, CHANNEL_TILES)
             column = CHANNEL_TILES * (u % HEADS) + m
-            a_t = a_pool.tile([P, BLOCK], F32)
+            a_part = a_of[u][:, m, :]
             tanh_t = tanh_pool.tile([P, BLOCK], F32)
-            for gate, target in ((GATE_A, a_t), (GATE_X, tanh_t)):
+            for gate, target in ((GATE_A, a_part), (GATE_X, tanh_t[:])):
                 nc.scalar.activation(
-                    out=target[:],
+                    out=target,
                     in_=sums_of[s, gate][:],
                     func=ACT.Tanh,
                     bias=half_bias[:, 8 * gate + column : 8 * gate + column + 1],
                     scale=0.5,
                 )
             nc.scalar.activation(
-                out=a_t[:],
-                in_=a_t[:],
+                out=a_part,
+                in_=a_part,
                 func=ACT.Exp,
                 bias=minus_4c[:, column : column + 1],
                 scale=minus_4c[:, column : column + 1],
             )
-            a_of[s], tanh_of[s] = a_t, tanh_t
+            tanh_of[s] = tanh_t
 
-        def square(s):
-            u, m = divmod(s, CHANNEL_TILES)
-            nc.gpsimd.tensor_tensor(
-                out=root_of[u][:, m, :], in0=a_of[s][:], in1=a_of[s][:], op=ALU.mult
-            )
+        def square(u):
+            nc.gpsimd.tensor_tensor(out=root_of[u][:], in0=a_of[u][:], in1=a_of[u][:], op=ALU.mult)
 
         def turn_back(source):
             turned = turn_pool.tile([P, ROW_TILES, P], F32, tag="turned")
@@ -217,7 +216,7 @@ def tile_rglru_t_e_kernel(
             b, h = divmod(u, HEADS)
             inside = slice(P * m, P * (m + 1))
             channels = slice(HEAD * h + P * m, HEAD * h + P * (m + 1))
-            a_rows = turn_back(a_of[s])
+            a_rows = turn_back(a_of[u][:, m, :])
             nc.vector.tensor_tensor(
                 out=result_of[u][:, :, inside],
                 in0=a_rows[:],
@@ -241,13 +240,16 @@ def tile_rglru_t_e_kernel(
                     out=root_part, in_=root_part, func=ACT.Sqrt, bias=quarter[:], scale=-0.25
                 )
 
-        def finish(u, m, adder):
+        def finish(u, m):
             inside = slice(P * m, P * (m + 1))
             root_rows = turn_back(root_of[u][:, m, :])
             fresh_part = fresh_of[u][:, :, inside]
-            result_part = result_of[u][:, :, inside]
             nc.vector.tensor_tensor(out=fresh_part, in0=root_rows[:], in1=fresh_part, op=ALU.mult)
-            adder.tensor_tensor(out=result_part, in0=result_part, in1=fresh_part, op=ALU.add)
+
+        def add(u, adder):
+            adder.tensor_tensor(
+                out=result_of[u][:], in0=result_of[u][:], in1=fresh_of[u][:], op=ALU.add
+            )
 
         def store(u):
             b, h = divmod(u, HEADS)
@@ -304,7 +306,8 @@ def tile_rglru_t_e_kernel(
             if m == STORE_STEP and done["store"] < len(finished):
                 store(finished[done["store"]])
                 done["store"] += 1
-            square(s)
+            if m == CHANNEL_TILES - 1:
+                square(u)
             if u % ROUND_UNITS == ROUND_UNITS - 1 and m == CHANNEL_TILES - 1:
                 last_round = u == UNITS - 1
                 passes_up_to(s + 2)
@@ -314,8 +317,9 @@ def tile_rglru_t_e_kernel(
                     roots(v)
                 for v in members:
                     for mm in range(CHANNEL_TILES):
-                        helper = last_round and mm % 2 == 1
-                        finish(v, mm, nc.vector if helper else nc.gpsimd)
+                        finish(v, mm)
+                    helper = last_round and v >= u + 1 - ROUND_UNITS // 2
+                    add(v, nc.vector if helper else nc.gpsimd)
                     finished.append(v)
                     if last_round:
                         for w in finished[done["store"] :]:

@@ -180,7 +180,7 @@ def tile_rglru_t_e_kernel(
                 )
                 sums_of[s, gate] = acc
 
-        def gates(s):
+        def gates(s, own_squares):
             u, m = divmod(s, CHANNEL_TILES)
             column = CHANNEL_TILES * (u % HEADS) + m
             a_part = a_of[u][:, m, :]
@@ -193,6 +193,8 @@ def tile_rglru_t_e_kernel(
                     bias=half_bias[:, 8 * gate + column : 8 * gate + column + 1],
                     scale=0.5,
                 )
+            if own_squares and m > 0:
+                square_on_scalar(u, m - 1)
             nc.scalar.activation(
                 out=a_part,
                 in_=a_part,
@@ -204,6 +206,14 @@ def tile_rglru_t_e_kernel(
 
         def square(u):
             nc.gpsimd.tensor_tensor(out=root_of[u][:], in0=a_of[u][:], in1=a_of[u][:], op=ALU.mult)
+
+        def square_on_scalar(u, m):
+            nc.scalar.activation(out=root_of[u][:, m, :], in_=a_of[u][:, m, :], func=ACT.Square)
+
+        def square_granule(u, m):
+            nc.gpsimd.tensor_tensor(
+                out=root_of[u][:, m, :], in0=a_of[u][:, m, :], in1=a_of[u][:, m, :], op=ALU.mult
+            )
 
         def turn_back(source):
             turned = turn_pool.tile([P, ROW_TILES, P], F32, tag="turned")
@@ -291,7 +301,8 @@ def tile_rglru_t_e_kernel(
             if m == 0:
                 open_unit(u)
             passes_up_to(s + 1)
-            gates(s)
+            own_squares = u % ROUND_UNITS == ROUND_UNITS - 1
+            gates(s, own_squares)
             keep_up_to(s - 1)
             if h == 0 and b + 1 < BLOCKS:
                 regroup(b + 1, m)
@@ -306,7 +317,9 @@ def tile_rglru_t_e_kernel(
             if m == STORE_STEP and done["store"] < len(finished):
                 store(finished[done["store"]])
                 done["store"] += 1
-            if m == CHANNEL_TILES - 1:
+            if u == 0:
+                square_granule(u, m)
+            elif m == CHANNEL_TILES - 1 and not own_squares:
                 square(u)
             if u % ROUND_UNITS == ROUND_UNITS - 1 and m == CHANNEL_TILES - 1:
                 last_round = u == UNITS - 1
@@ -315,6 +328,8 @@ def tile_rglru_t_e_kernel(
                 members = range(u + 1 - ROUND_UNITS, u + 1)
                 for v in members:
                     roots(v)
+                    if v == u + 1 - ROUND_UNITS:
+                        square_on_scalar(u, m)
                 for v in members:
                     for mm in range(CHANNEL_TILES):
                         finish(v, mm)

@@ -27,9 +27,11 @@ ROOT_TILES = 2
 UNITS = BLOCKS * HEADS
 STEPS = UNITS * CHANNEL_TILES
 ROUND_UNITS = 4
-X_BLOCKS = 3
+ROUND_BLOCKS = ROUND_UNITS // HEADS
+X_BLOCKS = 4
 A_UNITS = 4
 STORE_STEP = 2
+LATE_UNITS = 1
 
 FLOPS = 2 * ROWS * HEAD * HEAD * HEADS * 2
 
@@ -52,7 +54,7 @@ def tile_rglru_t_e_kernel(
         tanh_pool = ctx.enter_context(tc.tile_pool(name="tanh", bufs=4))
         root_pool = ctx.enter_context(tc.tile_pool(name="root", bufs=ROUND_UNITS))
         result_pool = ctx.enter_context(tc.tile_pool(name="result", bufs=ROUND_UNITS + 1))
-        fresh_pool = ctx.enter_context(tc.tile_pool(name="fresh", bufs=ROUND_UNITS + 1))
+        fresh_pool = ctx.enter_context(tc.tile_pool(name="fresh", bufs=ROUND_UNITS))
         sum_pool = ctx.enter_context(tc.psum_pool(name="sums", bufs=4))
         turn_pool = ctx.enter_context(tc.psum_pool(name="turned", bufs=4))
         ctx.enter_context(tc.manual_schedule())
@@ -277,12 +279,14 @@ def tile_rglru_t_e_kernel(
         )
         minus_4c = keep.tile([P, 8], F32)
         nc.vector.tensor_scalar_mul(out=minus_4c[:], in0=soft[:], scalar1=-4.0)
+        load_x(1)
         load_state(0)
-        for b in range(1, X_BLOCKS):
+        for b in range(2, X_BLOCKS):
             load_x(b)
         load_state(1)
 
-        done = {"passes": 0, "keep": 0, "store": 0}
+        done = {"passes": 0, "keep": 0, "store": 0, "late": 0}
+        late = []
 
         def passes_up_to(last):
             for s in range(done["passes"], min(last, STEPS - 1) + 1):
@@ -300,15 +304,25 @@ def tile_rglru_t_e_kernel(
             b, h = divmod(u, HEADS)
             if m == 0:
                 open_unit(u)
-            passes_up_to(s + 1)
+            round_end = (u // ROUND_UNITS + 1) * ROUND_UNITS * CHANNEL_TILES - 1
+            passes_up_to(min(s + 1, round_end))
             own_squares = u % ROUND_UNITS == ROUND_UNITS - 1
             gates(s, own_squares)
             keep_up_to(s - 1)
-            if h == 0 and b + 1 < BLOCKS:
-                regroup(b + 1, m)
-            if h == 1 and m == 1 and b + 1 < BLOCKS:
-                open_codes(b + 1)
-                quantise(b + 1, 0, HEADS)
+            if done["late"] < len(late):
+                v, mm = late[done["late"]]
+                done["late"] += 1
+                finish(v, mm)
+                if mm == CHANNEL_TILES - 1:
+                    add(v, nc.gpsimd)
+                    finished.append(v)
+            if u == 0:
+                regroup(1, m)
+            if u == 1 and m == 1:
+                open_codes(1)
+                quantise(1, 0, HEADS)
+            if h == HEADS - 1 and b + ROUND_BLOCKS < BLOCKS:
+                regroup(b + ROUND_BLOCKS, m)
             if h == 0 and m == 0 and b >= 1:
                 if b + X_BLOCKS - 1 < BLOCKS:
                     load_x(b + X_BLOCKS - 1)
@@ -323,17 +337,26 @@ def tile_rglru_t_e_kernel(
                 square(u)
             if u % ROUND_UNITS == ROUND_UNITS - 1 and m == CHANNEL_TILES - 1:
                 last_round = u == UNITS - 1
-                passes_up_to(s + 2)
                 keep_up_to(s)
+                for following in range(b + 1, min(b + 1 + ROUND_BLOCKS, BLOCKS)):
+                    open_codes(following)
+                    quantise(following, 0, HEADS)
+                passes_up_to(s + 2)
                 members = range(u + 1 - ROUND_UNITS, u + 1)
                 for v in members:
                     roots(v)
                     if v == u + 1 - ROUND_UNITS:
                         square_on_scalar(u, m)
                 for v in members:
+                    if not last_round and v > u - LATE_UNITS:
+                        late.extend([(v, mm) for mm in range(CHANNEL_TILES)])
+                        continue
                     for mm in range(CHANNEL_TILES):
                         finish(v, mm)
-                    helper = last_round and v >= u + 1 - ROUND_UNITS // 2
+                    if last_round:
+                        helper = v >= u + 1 - ROUND_UNITS // 2
+                    else:
+                        helper = v == u + 1 - ROUND_UNITS
                     add(v, nc.vector if helper else nc.gpsimd)
                     finished.append(v)
                     if last_round:

@@ -76,12 +76,15 @@ def tile_rglru_t_e_kernel(
             nc.sync.dma_start(out=state_sb[:], in_=state_blocks[b])
             state_of[b] = state_sb
 
+        x_first = x_pool.tile([P, ROW_TILES, CHANNELS], BF16, tag="x_sb")
+        x_of[0] = x_first
+        nc.sync.dma_start(out=x_first[:, :, 0:HEAD], in_=x_blocks[0][:, :, 0:HEAD])
         ident = keep.tile([P, P], F32)
         make_identity(nc, ident[:])
-        w_planes = keep.tile([P, 2 * HEADS, HEAD], U8, align_bytes=64)
-        nc.vector.memset(w_planes[:].bitcast(I32), 0)
         vector_rows = keep.tile([P, P], BF16)
         nc.vector.memset(vector_rows[:], 0.0)
+        w_planes = keep.tile([P, 2 * HEADS, HEAD], U8, align_bytes=64)
+        nc.vector.memset(w_planes[:].bitcast(I32), 0)
         quarter = keep.tile([P, 1], F32)
         nc.vector.memset(quarter[:], 0.25)
         one = keep.tile([P, 1], F32)
@@ -90,7 +93,7 @@ def tile_rglru_t_e_kernel(
         nc.sync.dma_start(out=vector_rows[0:8, :], in_=b_in.rearrange("h (m p) -> (h m) p", p=P))
         nc.sync.dma_start(out=vector_rows[8:16, :], in_=b_a.rearrange("h (m p) -> (h m) p", p=P))
         nc.sync.dma_start(out=vector_rows[16:24, :], in_=a_param.rearrange("(m p) -> m p", p=P))
-        load_x(0)
+        nc.sync.dma_start(out=x_first[:, :, HEAD:CHANNELS], in_=x_blocks[0][:, :, HEAD:CHANNELS])
         w_codes = keep.tile([P, 2 * HEADS, HEAD], I32, align_bytes=64)
         for gate, words in ((GATE_X, w_in_words), (GATE_A, w_a_words)):
             nc.sync.dma_start(
@@ -306,7 +309,7 @@ def tile_rglru_t_e_kernel(
                 open_unit(u)
             round_end = (u // ROUND_UNITS + 1) * ROUND_UNITS * CHANNEL_TILES - 1
             passes_up_to(min(s + 1, round_end))
-            own_squares = u % ROUND_UNITS == ROUND_UNITS - 1
+            own_squares = u % ROUND_UNITS == ROUND_UNITS - 1 and u < UNITS - 1
             gates(s, own_squares)
             keep_up_to(s - 1)
             if done["late"] < len(late):
@@ -345,7 +348,7 @@ def tile_rglru_t_e_kernel(
                 members = range(u + 1 - ROUND_UNITS, u + 1)
                 for v in members:
                     roots(v)
-                    if v == u + 1 - ROUND_UNITS:
+                    if v == u + 1 - ROUND_UNITS and not last_round:
                         square_on_scalar(u, m)
                 for v in members:
                     if not last_round and v > u - LATE_UNITS:

@@ -53,7 +53,7 @@ def tile_rglru_t_e_kernel(
         a_pool = ctx.enter_context(tc.tile_pool(name="a", bufs=A_UNITS))
         tanh_pool = ctx.enter_context(tc.tile_pool(name="tanh", bufs=4))
         root_pool = ctx.enter_context(tc.tile_pool(name="root", bufs=ROUND_UNITS))
-        result_pool = ctx.enter_context(tc.tile_pool(name="result", bufs=ROUND_UNITS + 1))
+        result_pool = ctx.enter_context(tc.tile_pool(name="result", bufs=ROUND_UNITS + 2))
         fresh_pool = ctx.enter_context(tc.tile_pool(name="fresh", bufs=ROUND_UNITS))
         sum_pool = ctx.enter_context(tc.psum_pool(name="sums", bufs=4))
         turn_pool = ctx.enter_context(tc.psum_pool(name="turned", bufs=4))
@@ -87,6 +87,7 @@ def tile_rglru_t_e_kernel(
         nc.vector.memset(w_planes[:].bitcast(I32), 0)
         quarter = keep.tile([P, 1], F32)
         nc.vector.memset(quarter[:], 0.25)
+        last_code = keep.tile([P, 1], U32)
         one = keep.tile([P, 1], F32)
         nc.vector.memset(one[:], 1.0)
 
@@ -185,7 +186,7 @@ def tile_rglru_t_e_kernel(
                 )
                 sums_of[s, gate] = acc
 
-        def gates(s, own_squares):
+        def gates(s):
             u, m = divmod(s, CHANNEL_TILES)
             column = CHANNEL_TILES * (u % HEADS) + m
             a_part = a_of[u][:, m, :]
@@ -198,8 +199,6 @@ def tile_rglru_t_e_kernel(
                     bias=half_bias[:, 8 * gate + column : 8 * gate + column + 1],
                     scale=0.5,
                 )
-            if own_squares and m > 0:
-                square_on_scalar(u, m - 1)
             nc.scalar.activation(
                 out=a_part,
                 in_=a_part,
@@ -212,8 +211,8 @@ def tile_rglru_t_e_kernel(
         def square(u):
             nc.gpsimd.tensor_tensor(out=root_of[u][:], in0=a_of[u][:], in1=a_of[u][:], op=ALU.mult)
 
-        def square_on_scalar(u, m):
-            nc.scalar.activation(out=root_of[u][:, m, :], in_=a_of[u][:, m, :], func=ACT.Square)
+        def follow_quantise(b):
+            nc.gpsimd.tensor_copy(out=last_code[:], in_=codes_of[b][:, 0:1])
 
         def square_granule(u, m):
             nc.gpsimd.tensor_tensor(
@@ -309,8 +308,15 @@ def tile_rglru_t_e_kernel(
                 open_unit(u)
             round_end = (u // ROUND_UNITS + 1) * ROUND_UNITS * CHANNEL_TILES - 1
             passes_up_to(min(s + 1, round_end))
-            own_squares = u % ROUND_UNITS == ROUND_UNITS - 1 and u < UNITS - 1
-            gates(s, own_squares)
+            round_last = u % ROUND_UNITS == ROUND_UNITS - 1 and u < UNITS - 1
+            gates(s)
+            if u % ROUND_UNITS == ROUND_UNITS - 1 and m == CHANNEL_TILES - 1:
+                for following in range(b + 1, min(b + 1 + ROUND_BLOCKS, BLOCKS)):
+                    open_codes(following)
+                    quantise(following, 0, HEADS)
+                if round_last:
+                    follow_quantise(b + ROUND_BLOCKS)
+                    square(u)
             keep_up_to(s - 1)
             if done["late"] < len(late):
                 v, mm = late[done["late"]]
@@ -324,8 +330,10 @@ def tile_rglru_t_e_kernel(
             if u == 1 and m == 1:
                 open_codes(1)
                 quantise(1, 0, HEADS)
-            if h == HEADS - 1 and b + ROUND_BLOCKS < BLOCKS:
-                regroup(b + ROUND_BLOCKS, m)
+            if (h, m) >= (0, CHANNEL_TILES - 1) and b + ROUND_BLOCKS < BLOCKS:
+                piece = CHANNEL_TILES * h + m - (CHANNEL_TILES - 1)
+                if piece < HEADS * ROW_TILES // 2:
+                    regroup(b + ROUND_BLOCKS, piece)
             if h == 0 and m == 0 and b >= 1:
                 if b + X_BLOCKS - 1 < BLOCKS:
                     load_x(b + X_BLOCKS - 1)
@@ -336,20 +344,15 @@ def tile_rglru_t_e_kernel(
                 done["store"] += 1
             if u == 0:
                 square_granule(u, m)
-            elif m == CHANNEL_TILES - 1 and not own_squares:
+            elif m == CHANNEL_TILES - 1 and not round_last:
                 square(u)
             if u % ROUND_UNITS == ROUND_UNITS - 1 and m == CHANNEL_TILES - 1:
                 last_round = u == UNITS - 1
                 keep_up_to(s)
-                for following in range(b + 1, min(b + 1 + ROUND_BLOCKS, BLOCKS)):
-                    open_codes(following)
-                    quantise(following, 0, HEADS)
                 passes_up_to(s + 2)
                 members = range(u + 1 - ROUND_UNITS, u + 1)
                 for v in members:
                     roots(v)
-                    if v == u + 1 - ROUND_UNITS and not last_round:
-                        square_on_scalar(u, m)
                 for v in members:
                     if not last_round and v > u - LATE_UNITS:
                         late.extend([(v, mm) for mm in range(CHANNEL_TILES)])

@@ -26,11 +26,15 @@ GATE_X, GATE_A = 0, 1
 ROOT_TILES = 2
 UNITS = BLOCKS * HEADS
 STEPS = UNITS * CHANNEL_TILES
-ROUND_UNITS = 4
-ROUND_BLOCKS = ROUND_UNITS // HEADS
+ROUNDS = (4, 4, 4, 4)
+ROUND_UNITS = max(ROUNDS)
+FEED_UNITS = 4
+FEED_BLOCKS = FEED_UNITS // HEADS
 X_BLOCKS = 4
 A_UNITS = 4
 STORE_STEP = 2
+ALL_TILES = slice(0, ROW_TILES)
+HALVES = (slice(0, ROW_TILES // 2), slice(ROW_TILES // 2, ROW_TILES))
 LATE_UNITS = 1
 
 FLOPS = 2 * ROWS * HEAD * HEAD * HEADS * 2
@@ -260,16 +264,14 @@ def tile_rglru_t_e_kernel(
             fresh_part = fresh_of[u][:, :, inside]
             nc.vector.tensor_tensor(out=fresh_part, in0=root_rows[:], in1=fresh_part, op=ALU.mult)
 
-        def add(u, adder):
-            adder.tensor_tensor(
-                out=result_of[u][:], in0=result_of[u][:], in1=fresh_of[u][:], op=ALU.add
-            )
+        def add(u, adder, tiles=ALL_TILES):
+            part = result_of[u][:, tiles, :]
+            adder.tensor_tensor(out=part, in0=part, in1=fresh_of[u][:, tiles, :], op=ALU.add)
 
-        def store(u):
+        def store(u, tiles=ALL_TILES):
             b, h = divmod(u, HEADS)
-            nc.sync.dma_start(
-                out=out_blocks[b][:, :, HEAD * h : HEAD * (h + 1)], in_=result_of[u][:]
-            )
+            channels = slice(HEAD * h, HEAD * (h + 1))
+            nc.sync.dma_start(out=out_blocks[b][:, tiles, channels], in_=result_of[u][:, tiles, :])
 
         open_codes(0)
         for h in range(HEADS):
@@ -300,40 +302,46 @@ def tile_rglru_t_e_kernel(
                 keep_granule(s)
                 done["keep"] = s + 1
 
+        to_add = []
         finished = []
+        members_of = {}
+        first = 0
+        for units in ROUNDS:
+            for u in range(first, first + units):
+                members_of[u] = range(first, first + units)
+            first += units
         for s in range(STEPS):
             u, m = divmod(s, CHANNEL_TILES)
             b, h = divmod(u, HEADS)
+            members = members_of[u]
+            unit_end = m == CHANNEL_TILES - 1
+            feed_end = unit_end and u % FEED_UNITS == FEED_UNITS - 1 and u < UNITS - 1
             if m == 0:
                 open_unit(u)
-            round_end = (u // ROUND_UNITS + 1) * ROUND_UNITS * CHANNEL_TILES - 1
-            passes_up_to(min(s + 1, round_end))
-            round_last = u % ROUND_UNITS == ROUND_UNITS - 1 and u < UNITS - 1
+            passes_up_to(min(s + 1, CHANNEL_TILES * members.stop - 1))
             gates(s)
-            if u % ROUND_UNITS == ROUND_UNITS - 1 and m == CHANNEL_TILES - 1:
-                for following in range(b + 1, min(b + 1 + ROUND_BLOCKS, BLOCKS)):
+            if feed_end:
+                for following in range(b + 1, b + 1 + FEED_BLOCKS):
                     open_codes(following)
                     quantise(following, 0, HEADS)
-                if round_last:
-                    follow_quantise(b + ROUND_BLOCKS)
-                    square(u)
+                follow_quantise(b + FEED_BLOCKS)
+                square(u)
             keep_up_to(s - 1)
             if done["late"] < len(late):
                 v, mm = late[done["late"]]
                 done["late"] += 1
                 finish(v, mm)
                 if mm == CHANNEL_TILES - 1:
-                    add(v, nc.gpsimd)
-                    finished.append(v)
+                    to_add.append(v)
             if u == 0:
                 regroup(1, m)
             if u == 1 and m == 1:
                 open_codes(1)
                 quantise(1, 0, HEADS)
-            if (h, m) >= (0, CHANNEL_TILES - 1) and b + ROUND_BLOCKS < BLOCKS:
+            if (h, m) >= (0, CHANNEL_TILES - 1) and b + FEED_BLOCKS < BLOCKS:
                 piece = CHANNEL_TILES * h + m - (CHANNEL_TILES - 1)
                 if piece < HEADS * ROW_TILES // 2:
-                    regroup(b + ROUND_BLOCKS, piece)
+                    regroup(b + FEED_BLOCKS, piece)
             if h == 0 and m == 0 and b >= 1:
                 if b + X_BLOCKS - 1 < BLOCKS:
                     load_x(b + X_BLOCKS - 1)
@@ -342,30 +350,37 @@ def tile_rglru_t_e_kernel(
             if m == STORE_STEP and done["store"] < len(finished):
                 store(finished[done["store"]])
                 done["store"] += 1
-            if u == 0:
+            if u == 0 or u == UNITS - 1:
                 square_granule(u, m)
-            elif m == CHANNEL_TILES - 1 and not round_last:
+            elif unit_end and not feed_end:
                 square(u)
-            if u % ROUND_UNITS == ROUND_UNITS - 1 and m == CHANNEL_TILES - 1:
-                last_round = u == UNITS - 1
+            for v in to_add:
+                add(v, nc.gpsimd)
+            finished.extend(to_add)
+            to_add.clear()
+            if unit_end and u == members[-1]:
                 keep_up_to(s)
-                passes_up_to(s + 2)
-                members = range(u + 1 - ROUND_UNITS, u + 1)
-                for v in members:
-                    roots(v)
-                for v in members:
-                    if not last_round and v > u - LATE_UNITS:
-                        late.extend([(v, mm) for mm in range(CHANNEL_TILES)])
-                        continue
-                    for mm in range(CHANNEL_TILES):
-                        finish(v, mm)
-                    if last_round:
-                        helper = v >= u + 1 - ROUND_UNITS // 2
-                    else:
-                        helper = v == u + 1 - ROUND_UNITS
-                    add(v, nc.vector if helper else nc.gpsimd)
-                    finished.append(v)
-                    if last_round:
-                        for w in finished[done["store"] :]:
-                            store(w)
-                        done["store"] = len(finished)
+                if u < UNITS - 1:
+                    passes_up_to(s + 2)
+                    for v in members:
+                        roots(v)
+                    for v in members[:-1]:
+                        for mm in range(CHANNEL_TILES):
+                            finish(v, mm)
+                        add(v, nc.vector if v == members[0] else nc.gpsimd)
+                        finished.append(v)
+                    late.extend([(u, mm) for mm in range(CHANNEL_TILES)])
+        for v in finished[done["store"] :]:
+            store(v)
+        for v in members:
+            roots(v)
+        for v in members[:-1]:
+            for mm in range(CHANNEL_TILES):
+                finish(v, mm)
+            add(v, nc.gpsimd if v == members[0] else nc.vector)
+            store(v)
+        for mm in range(CHANNEL_TILES):
+            finish(members[-1], mm)
+        for tiles in HALVES:
+            add(members[-1], nc.vector, tiles)
+            store(members[-1], tiles)

@@ -26,16 +26,13 @@ GATE_X, GATE_A = 0, 1
 ROOT_TILES = 2
 UNITS = BLOCKS * HEADS
 STEPS = UNITS * CHANNEL_TILES
-ROUNDS = (4, 4, 4, 4)
+ROUNDS = (5, 5, 4, 2)
 ROUND_UNITS = max(ROUNDS)
-FEED_UNITS = 4
-FEED_BLOCKS = FEED_UNITS // HEADS
 X_BLOCKS = 4
-A_UNITS = 4
-STORE_STEP = 2
+STATE_BLOCKS = 2
+STORE_STEPS = (1, 3)
 ALL_TILES = slice(0, ROW_TILES)
 HALVES = (slice(0, ROW_TILES // 2), slice(ROW_TILES // 2, ROW_TILES))
-LATE_UNITS = 1
 
 FLOPS = 2 * ROWS * HEAD * HEAD * HEADS * 2
 
@@ -51,13 +48,12 @@ def tile_rglru_t_e_kernel(
     with ExitStack() as ctx:
         keep = ctx.enter_context(tc.tile_pool(name="keep", bufs=1))
         x_pool = ctx.enter_context(tc.tile_pool(name="x", bufs=X_BLOCKS))
-        state_pool = ctx.enter_context(tc.tile_pool(name="state", bufs=2))
-        grouped_pool = ctx.enter_context(tc.tile_pool(name="grouped", bufs=2))
-        code_pool = ctx.enter_context(tc.tile_pool(name="codes", bufs=2))
-        a_pool = ctx.enter_context(tc.tile_pool(name="a", bufs=A_UNITS))
-        tanh_pool = ctx.enter_context(tc.tile_pool(name="tanh", bufs=4))
-        root_pool = ctx.enter_context(tc.tile_pool(name="root", bufs=ROUND_UNITS))
-        result_pool = ctx.enter_context(tc.tile_pool(name="result", bufs=ROUND_UNITS + 2))
+        state_pool = ctx.enter_context(tc.tile_pool(name="state", bufs=STATE_BLOCKS))
+        grouped_pool = ctx.enter_context(tc.tile_pool(name="grouped", bufs=ROUND_UNITS))
+        code_pool = ctx.enter_context(tc.tile_pool(name="codes", bufs=ROUND_UNITS + 1))
+        a_pool = ctx.enter_context(tc.tile_pool(name="a", bufs=ROUND_UNITS + 1))
+        tanh_pool = ctx.enter_context(tc.tile_pool(name="tanh", bufs=3))
+        result_pool = ctx.enter_context(tc.tile_pool(name="result", bufs=ROUND_UNITS + 1))
         fresh_pool = ctx.enter_context(tc.tile_pool(name="fresh", bufs=ROUND_UNITS))
         sum_pool = ctx.enter_context(tc.psum_pool(name="sums", bufs=4))
         turn_pool = ctx.enter_context(tc.psum_pool(name="turned", bufs=4))
@@ -65,24 +61,27 @@ def tile_rglru_t_e_kernel(
 
         x_of, state_of = {}, {}
         grouped_of, codes_of, planes_of = {}, {}, {}
-        sums_of, tanh_of = {}, {}
         a_of, root_of, result_of, fresh_of = {}, {}, {}, {}
+        sums_of, tanh_of = {}, {}
+
+        def load_x_head(b, h):
+            channels = slice(HEAD * h, HEAD * (h + 1))
+            nc.sync.dma_start(out=x_of[b][:, h, :, :], in_=x_blocks[b][:, :, channels])
 
         def load_x(b):
-            x_sb = x_pool.tile([P, ROW_TILES, CHANNELS], BF16)
-            for h in range(HEADS):
-                channels = slice(HEAD * h, HEAD * (h + 1))
-                nc.sync.dma_start(out=x_sb[:, :, channels], in_=x_blocks[b][:, :, channels])
+            x_sb = x_pool.tile([P, HEADS, ROW_TILES, HEAD], BF16)
             x_of[b] = x_sb
+            for h in range(HEADS):
+                load_x_head(b, h)
 
         def load_state(b):
             state_sb = state_pool.tile([P, ROW_TILES, CHANNELS], BF16)
             nc.sync.dma_start(out=state_sb[:], in_=state_blocks[b])
             state_of[b] = state_sb
 
-        x_first = x_pool.tile([P, ROW_TILES, CHANNELS], BF16, tag="x_sb")
+        x_first = x_pool.tile([P, HEADS, ROW_TILES, HEAD], BF16, tag="x_sb")
         x_of[0] = x_first
-        nc.sync.dma_start(out=x_first[:, :, 0:HEAD], in_=x_blocks[0][:, :, 0:HEAD])
+        load_x_head(0, 0)
         ident = keep.tile([P, P], F32)
         make_identity(nc, ident[:])
         vector_rows = keep.tile([P, P], BF16)
@@ -98,7 +97,7 @@ def tile_rglru_t_e_kernel(
         nc.sync.dma_start(out=vector_rows[0:8, :], in_=b_in.rearrange("h (m p) -> (h m) p", p=P))
         nc.sync.dma_start(out=vector_rows[8:16, :], in_=b_a.rearrange("h (m p) -> (h m) p", p=P))
         nc.sync.dma_start(out=vector_rows[16:24, :], in_=a_param.rearrange("(m p) -> m p", p=P))
-        nc.sync.dma_start(out=x_first[:, :, HEAD:CHANNELS], in_=x_blocks[0][:, :, HEAD:CHANNELS])
+        load_x_head(0, 1)
         w_codes = keep.tile([P, 2 * HEADS, HEAD], I32, align_bytes=64)
         for gate, words in ((GATE_X, w_in_words), (GATE_A, w_a_words)):
             nc.sync.dma_start(
@@ -129,62 +128,61 @@ def tile_rglru_t_e_kernel(
         nc.scalar.activation(out=soft[:], in_=soft[:], func=ACT.Exp, scale=-1.0)
         nc.scalar.activation(out=soft[:], in_=soft[:], func=ACT.Ln, bias=one[:])
 
-        def regroup(b, piece):
-            h, pair = divmod(piece, ROW_TILES // 2)
-            if piece == 0:
-                grouped = grouped_pool.tile([P, HEADS, BLOCK, PACK], BF16, align_bytes=64)
-                grouped_of[b] = grouped
+        def regroup(u, pair):
+            if pair == 0:
+                grouped = grouped_pool.tile([P, BLOCK, PACK], BF16, align_bytes=64)
+                grouped_of[u] = grouped
+            b, h = divmod(u, HEADS)
             x_words = x_of[b][:].bitcast(F32)
-            grouped_words = grouped_of[b][:].bitcast(F32)
+            grouped_words = grouped_of[u][:].bitcast(F32)
             turned = turn_pool.tile([P, 2, 2, P], F32, tag="turned")
             for i in range(2):
                 for w in range(2):
                     nc.tensor.transpose(
                         turned[:, i, w, :],
-                        x_words[:, 2 * pair + i, 256 * h + w : 256 * (h + 1) : 2],
+                        x_words[:, h, 2 * pair + i, w : HEAD // 2 : 2],
                         ident[:],
                     )
             nc.vector.tensor_copy(
-                out=grouped_words[:, h, 2 * P * pair : 2 * P * (pair + 1), :].rearrange(
+                out=grouped_words[:, 2 * P * pair : 2 * P * (pair + 1), :].rearrange(
                     "p (i r) w -> p i r w", i=2
                 ),
                 in_=turned[:].rearrange("p i w r -> p i r w"),
             )
 
-        def open_codes(b):
-            codes = code_pool.tile([P, HEADS * BLOCK], U32, align_bytes=64)
-            plane = code_pool.tile([P, HEADS * BLOCK], U8, align_bytes=64)
-            codes_of[b], planes_of[b] = codes, plane
-
-        def quantise(b, first, heads):
-            columns = slice(BLOCK * first, BLOCK * (first + heads))
+        def quantise(u):
+            codes = code_pool.tile([P, BLOCK], U32, align_bytes=64)
+            plane = code_pool.tile([P, BLOCK], U8, align_bytes=64)
+            codes_of[u], planes_of[u] = codes, plane
             nc.vector.quantize_mx(
-                out=codes_of[b][:, columns].bitcast(FP8X4),
-                scales=planes_of[b][:, columns],
-                in_=grouped_of[b][:, first : first + heads, :, :].rearrange("p h r t -> p (h r t)"),
+                out=codes[:].bitcast(FP8X4),
+                scales=plane[:],
+                in_=grouped_of[u][:].rearrange("p r t -> p (r t)"),
             )
 
         def open_unit(u):
             a_t = a_pool.tile([P, CHANNEL_TILES, BLOCK], F32)
             a_of[u] = a_t
-            root_t = root_pool.tile([P, CHANNEL_TILES, BLOCK], F32)
             result = result_pool.tile([P, ROW_TILES, HEAD], F32)
             fresh = fresh_pool.tile([P, ROW_TILES, HEAD], F32)
-            root_of[u], result_of[u], fresh_of[u] = root_t, result, fresh
+            result_of[u], fresh_of[u] = result, fresh
+            root_of[u] = a_t
+            if u == UNITS - 1:
+                root_t = result_pool.tile([P, CHANNEL_TILES, BLOCK], F32, tag="result")
+                root_of[u] = root_t
 
         def passes(s):
             u, m = divmod(s, CHANNEL_TILES)
-            b, h = divmod(u, HEADS)
+            h = u % HEADS
             channels = slice(P * m, P * (m + 1))
-            rows = slice(BLOCK * h, BLOCK * (h + 1))
             for gate in (GATE_A, GATE_X):
                 acc = sum_pool.tile([P, BLOCK], F32)
                 nc.tensor.matmul_mx(
                     out=acc[:],
                     lhsT=w_codes[:, HEADS * gate + h, channels].bitcast(FP8X4),
                     lhsT_scale=w_planes[:, HEADS * gate + h, channels],
-                    rhs=codes_of[b][:, rows].bitcast(FP8X4),
-                    rhs_scale=planes_of[b][:, rows],
+                    rhs=codes_of[u][:].bitcast(FP8X4),
+                    rhs_scale=planes_of[u][:],
                     start=True,
                     stop=True,
                 )
@@ -215,13 +213,12 @@ def tile_rglru_t_e_kernel(
         def square(u):
             nc.gpsimd.tensor_tensor(out=root_of[u][:], in0=a_of[u][:], in1=a_of[u][:], op=ALU.mult)
 
-        def follow_quantise(b):
-            nc.gpsimd.tensor_copy(out=last_code[:], in_=codes_of[b][:, 0:1])
+        def follow_quantise(u):
+            nc.gpsimd.tensor_copy(out=last_code[:], in_=codes_of[u][:, 0:1])
 
         def square_granule(u, m):
-            nc.gpsimd.tensor_tensor(
-                out=root_of[u][:, m, :], in0=a_of[u][:, m, :], in1=a_of[u][:, m, :], op=ALU.mult
-            )
+            part = a_of[u][:, m, :]
+            nc.gpsimd.tensor_tensor(out=root_of[u][:, m, :], in0=part, in1=part, op=ALU.mult)
 
         def turn_back(source):
             turned = turn_pool.tile([P, ROW_TILES, P], F32, tag="turned")
@@ -246,7 +243,7 @@ def tile_rglru_t_e_kernel(
                 out=fresh_of[u][:, :, inside],
                 in0=tanh_rows[:],
                 scalar=1.0,
-                in1=x_of[b][:, :, channels],
+                in1=x_of[b][:, h, :, inside],
                 op0=ALU.add,
                 op1=ALU.mult,
             )
@@ -273,11 +270,10 @@ def tile_rglru_t_e_kernel(
             channels = slice(HEAD * h, HEAD * (h + 1))
             nc.sync.dma_start(out=out_blocks[b][:, tiles, channels], in_=result_of[u][:, tiles, :])
 
-        open_codes(0)
-        for h in range(HEADS):
+        for u in range(HEADS):
             for pair in range(ROW_TILES // 2):
-                regroup(0, (ROW_TILES // 2) * h + pair)
-            quantise(0, h, 1)
+                regroup(u, pair)
+            quantise(u)
         nc.vector.scalar_tensor_tensor(
             out=soft[:], in0=a_par[:], scalar=0.0, in1=soft[:], op0=ALU.max, op1=ALU.add
         )
@@ -302,30 +298,41 @@ def tile_rglru_t_e_kernel(
                 keep_granule(s)
                 done["keep"] = s + 1
 
-        to_add = []
-        finished = []
         members_of = {}
+        regroup_at = {}
+        quantise_at = {4: (2, 3), 6: (4,)}
         first = 0
-        for units in ROUNDS:
-            for u in range(first, first + units):
-                members_of[u] = range(first, first + units)
+        for r, units in enumerate(ROUNDS):
+            members = range(first, first + units)
+            for u in members:
+                members_of[u] = members
+            following = range(members.stop, members.stop + ROUNDS[r + 1]) if r + 1 < len(ROUNDS) else ()
+            pieces = [(u, pair) for u in following for pair in range(ROW_TILES // 2)]
+            last = CHANNEL_TILES * members.stop - 2
+            start = max(CHANNEL_TILES * first, 8)
+            for i, piece in enumerate(pieces):
+                regroup_at[last - (last - start) * (len(pieces) - 1 - i) // len(pieces)] = piece
+            if r == 0:
+                for i in range(6):
+                    regroup_at[1 + i] = (2 + i // 2, i % 2)
             first += units
+        finished = []
+        to_add = []
+        to_square = []
         for s in range(STEPS):
             u, m = divmod(s, CHANNEL_TILES)
-            b, h = divmod(u, HEADS)
             members = members_of[u]
-            unit_end = m == CHANNEL_TILES - 1
-            feed_end = unit_end and u % FEED_UNITS == FEED_UNITS - 1 and u < UNITS - 1
+            round_end = s == CHANNEL_TILES * members.stop - 1
+            last_round = members.stop == UNITS
             if m == 0:
                 open_unit(u)
             passes_up_to(min(s + 1, CHANNEL_TILES * members.stop - 1))
             gates(s)
-            if feed_end:
-                for following in range(b + 1, b + 1 + FEED_BLOCKS):
-                    open_codes(following)
-                    quantise(following, 0, HEADS)
-                follow_quantise(b + FEED_BLOCKS)
-                square(u)
+            if round_end and not last_round:
+                following = members_of[u + 1] if u + 1 in members_of else ()
+                for v in following:
+                    quantise(v)
+                follow_quantise(following[-1])
             keep_up_to(s - 1)
             if done["late"] < len(late):
                 v, mm = late[done["late"]]
@@ -333,43 +340,51 @@ def tile_rglru_t_e_kernel(
                 finish(v, mm)
                 if mm == CHANNEL_TILES - 1:
                     to_add.append(v)
-            if u == 0:
-                regroup(1, m)
-            if u == 1 and m == 1:
-                open_codes(1)
-                quantise(1, 0, HEADS)
-            if (h, m) >= (0, CHANNEL_TILES - 1) and b + FEED_BLOCKS < BLOCKS:
-                piece = CHANNEL_TILES * h + m - (CHANNEL_TILES - 1)
-                if piece < HEADS * ROW_TILES // 2:
-                    regroup(b + FEED_BLOCKS, piece)
+            if s in regroup_at:
+                regroup(*regroup_at[s])
+            for v in quantise_at.get(s, ()):
+                quantise(v)
+            b, h = divmod(u, HEADS)
             if h == 0 and m == 0 and b >= 1:
-                if b + X_BLOCKS - 1 < BLOCKS:
-                    load_x(b + X_BLOCKS - 1)
-                if b + 1 < BLOCKS:
-                    load_state(b + 1)
-            if m == STORE_STEP and done["store"] < len(finished):
+                if b - 1 + X_BLOCKS < BLOCKS:
+                    load_x(b - 1 + X_BLOCKS)
+                if b - 1 + STATE_BLOCKS < BLOCKS:
+                    load_state(b - 1 + STATE_BLOCKS)
+            if m in STORE_STEPS and done["store"] < len(finished):
                 store(finished[done["store"]])
                 done["store"] += 1
-            if u == 0 or u == UNITS - 1:
+            if m == 0 and to_square:
+                square(to_square.pop())
+            if s in range(1, CHANNEL_TILES):
+                square_granule(u, m - 1)
+            if u == UNITS - 1:
                 square_granule(u, m)
-            elif unit_end and not feed_end:
-                square(u)
-            for v in to_add:
-                add(v, nc.gpsimd)
-            finished.extend(to_add)
-            to_add.clear()
-            if unit_end and u == members[-1]:
+            if s == CHANNEL_TILES:
+                square_granule(0, m + CHANNEL_TILES - 1)
+            if not last_round:
+                for v in to_add:
+                    add(v, nc.gpsimd)
+                finished.extend(to_add)
+                to_add.clear()
+            if m == CHANNEL_TILES - 1 and not round_end and u > 0:
+                to_square.append(u)
+            if round_end:
                 keep_up_to(s)
-                if u < UNITS - 1:
-                    passes_up_to(s + 2)
-                    for v in members:
-                        roots(v)
-                    for v in members[:-1]:
-                        for mm in range(CHANNEL_TILES):
-                            finish(v, mm)
-                        add(v, nc.vector if v == members[0] else nc.gpsimd)
-                        finished.append(v)
-                    late.extend([(u, mm) for mm in range(CHANNEL_TILES)])
+                if last_round:
+                    continue
+                square(u)
+                passes_up_to(s + 2)
+                for v in members:
+                    roots(v)
+                for v in members[:-1]:
+                    for mm in range(CHANNEL_TILES):
+                        finish(v, mm)
+                    add(v, nc.gpsimd)
+                    finished.append(v)
+                late.extend([(u, mm) for mm in range(CHANNEL_TILES)])
+        for v in to_add:
+            add(v, nc.gpsimd)
+        finished.extend(to_add)
         for v in finished[done["store"] :]:
             store(v)
         for v in members:
@@ -377,7 +392,7 @@ def tile_rglru_t_e_kernel(
         for v in members[:-1]:
             for mm in range(CHANNEL_TILES):
                 finish(v, mm)
-            add(v, nc.gpsimd if v == members[0] else nc.vector)
+            add(v, nc.vector)
             store(v)
         for mm in range(CHANNEL_TILES):
             finish(members[-1], mm)

@@ -26,7 +26,7 @@ GATE_X, GATE_A = 0, 1
 ROOT_TILES = 2
 UNITS = BLOCKS * HEADS
 STEPS = UNITS * CHANNEL_TILES
-ROUNDS = (5, 5, 4, 2)
+ROUNDS = (5, 5, 5, 1)
 ROUND_UNITS = max(ROUNDS)
 X_BLOCKS = 4
 STATE_BLOCKS = 2
@@ -164,11 +164,11 @@ def tile_rglru_t_e_kernel(
             a_t = a_pool.tile([P, CHANNEL_TILES, BLOCK], F32)
             a_of[u] = a_t
             result = result_pool.tile([P, ROW_TILES, HEAD], F32)
-            fresh = fresh_pool.tile([P, ROW_TILES, HEAD], F32)
+            fresh = fresh_pool.tile([P, CHANNEL_TILES, ROW_TILES, P], F32)
             result_of[u], fresh_of[u] = result, fresh
             root_of[u] = a_t
             if u == UNITS - 1:
-                root_t = result_pool.tile([P, CHANNEL_TILES, BLOCK], F32, tag="result")
+                root_t = a_pool.tile([P, CHANNEL_TILES, BLOCK], F32, tag="a_t")
                 root_of[u] = root_t
 
         def passes(s):
@@ -216,6 +216,9 @@ def tile_rglru_t_e_kernel(
         def follow_quantise(u):
             nc.gpsimd.tensor_copy(out=last_code[:], in_=codes_of[u][:, 0:1])
 
+        def square_on_scalar(u, m):
+            nc.scalar.activation(out=root_of[u][:, m, :], in_=a_of[u][:, m, :], func=ACT.Square)
+
         def square_granule(u, m):
             part = a_of[u][:, m, :]
             nc.gpsimd.tensor_tensor(out=root_of[u][:, m, :], in0=part, in1=part, op=ALU.mult)
@@ -240,7 +243,7 @@ def tile_rglru_t_e_kernel(
             )
             tanh_rows = turn_back(tanh_of[s])
             nc.vector.scalar_tensor_tensor(
-                out=fresh_of[u][:, :, inside],
+                out=fresh_of[u][:, m, :, :],
                 in0=tanh_rows[:],
                 scalar=1.0,
                 in1=x_of[b][:, h, :, inside],
@@ -256,14 +259,14 @@ def tile_rglru_t_e_kernel(
                 )
 
         def finish(u, m):
-            inside = slice(P * m, P * (m + 1))
             root_rows = turn_back(root_of[u][:, m, :])
-            fresh_part = fresh_of[u][:, :, inside]
+            fresh_part = fresh_of[u][:, m, :, :]
             nc.vector.tensor_tensor(out=fresh_part, in0=root_rows[:], in1=fresh_part, op=ALU.mult)
 
         def add(u, adder, tiles=ALL_TILES):
-            part = result_of[u][:, tiles, :]
-            adder.tensor_tensor(out=part, in0=part, in1=fresh_of[u][:, tiles, :], op=ALU.add)
+            part = result_of[u][:, tiles, :].rearrange("p t (m c) -> p t m c", c=P)
+            fresh_part = fresh_of[u][:, :, tiles, :].rearrange("p m t c -> p t m c")
+            adder.tensor_tensor(out=part, in0=part, in1=fresh_part, op=ALU.add)
 
         def store(u, tiles=ALL_TILES):
             b, h = divmod(u, HEADS)
@@ -328,6 +331,8 @@ def tile_rglru_t_e_kernel(
                 open_unit(u)
             passes_up_to(min(s + 1, CHANNEL_TILES * members.stop - 1))
             gates(s)
+            if last_round and m > 0:
+                square_on_scalar(u, m - 1)
             if round_end and not last_round:
                 following = members_of[u + 1] if u + 1 in members_of else ()
                 for v in following:
@@ -357,8 +362,6 @@ def tile_rglru_t_e_kernel(
                 square(to_square.pop())
             if s in range(1, CHANNEL_TILES):
                 square_granule(u, m - 1)
-            if u == UNITS - 1:
-                square_granule(u, m)
             if s == CHANNEL_TILES:
                 square_granule(0, m + CHANNEL_TILES - 1)
             if not last_round:
@@ -382,20 +385,16 @@ def tile_rglru_t_e_kernel(
                     add(v, nc.gpsimd)
                     finished.append(v)
                 late.extend([(u, mm) for mm in range(CHANNEL_TILES)])
-        for v in to_add:
-            add(v, nc.gpsimd)
-        finished.extend(to_add)
+        u = UNITS - 1
+        square_on_scalar(u, CHANNEL_TILES - 1)
         for v in finished[done["store"] :]:
             store(v)
-        for v in members:
-            roots(v)
-        for v in members[:-1]:
-            for mm in range(CHANNEL_TILES):
-                finish(v, mm)
+        roots(u)
+        for mm in range(CHANNEL_TILES):
+            finish(u, mm)
+        for v in to_add:
             add(v, nc.vector)
             store(v)
-        for mm in range(CHANNEL_TILES):
-            finish(members[-1], mm)
         for tiles in HALVES:
-            add(members[-1], nc.vector, tiles)
-            store(members[-1], tiles)
+            add(u, nc.vector, tiles)
+            store(u, tiles)

@@ -63,6 +63,7 @@ def tile_rglru_t_e_kernel(
         grouped_of, codes_of, planes_of = {}, {}, {}
         a_of, root_of, result_of, fresh_of = {}, {}, {}, {}
         sums_of, tanh_of = {}, {}
+        kept_of, new_of, sums_out_of = {}, {}, {}
 
         def load_x_head(b, h):
             channels = slice(HEAD * h, HEAD * (h + 1))
@@ -84,6 +85,8 @@ def tile_rglru_t_e_kernel(
         load_x_head(0, 0)
         ident = keep.tile([P, P], F32)
         make_identity(nc, ident[:])
+        ident_bf16 = keep.tile([P, P], BF16)
+        make_identity(nc, ident_bf16[:])
         vector_rows = keep.tile([P, P], BF16)
         nc.vector.memset(vector_rows[:], 0.0)
         w_planes = keep.tile([P, 2 * HEADS, HEAD], U8, align_bytes=64)
@@ -97,13 +100,16 @@ def tile_rglru_t_e_kernel(
         nc.sync.dma_start(out=vector_rows[0:8, :], in_=b_in.rearrange("h (m p) -> (h m) p", p=P))
         nc.sync.dma_start(out=vector_rows[8:16, :], in_=b_a.rearrange("h (m p) -> (h m) p", p=P))
         nc.sync.dma_start(out=vector_rows[16:24, :], in_=a_param.rearrange("(m p) -> m p", p=P))
-        load_x_head(0, 1)
         w_codes = keep.tile([P, 2 * HEADS, HEAD], I32, align_bytes=64)
-        for gate, words in ((GATE_X, w_in_words), (GATE_A, w_a_words)):
-            nc.sync.dma_start(
-                out=w_codes[:, HEADS * gate : HEADS * (gate + 1), :],
-                in_=words.rearrange("g p n t -> p g (n t)").bitcast(I32),
-            )
+
+        def load_weights(h):
+            for gate, words in ((GATE_A, w_a_words), (GATE_X, w_in_words)):
+                nc.sync.dma_start(
+                    out=w_codes[:, HEADS * gate + h, :],
+                    in_=words[h].rearrange("p n t -> p (n t)").bitcast(I32),
+                )
+
+        load_weights(0)
         for gate, scales in ((GATE_X, w_in_scales), (GATE_A, w_a_scales)):
             for quadrant in range(4):
                 nc.sync.dma_start(
@@ -115,16 +121,17 @@ def tile_rglru_t_e_kernel(
                     .bitcast(I32),
                 )
 
-        vector_f32 = keep.tile([P, P], F32)
-        nc.vector.tensor_copy(out=vector_f32[:], in_=vector_rows[:])
-        vector_cols = turn_pool.tile([P, HEAD], F32, tag="turned")
-        nc.tensor.transpose(vector_cols[:, 0:P], vector_f32[:], ident[:])
+        load_x_head(0, 1)
+        load_weights(1)
+
+        vector_cols = turn_pool.tile([P, P], BF16, tag="turned")
+        nc.tensor.transpose(vector_cols[:], vector_rows[:], ident_bf16[:])
         half_bias = keep.tile([P, 16], F32)
         nc.vector.tensor_scalar_mul(out=half_bias[:], in0=vector_cols[:, 0:16], scalar1=0.5)
         a_par = keep.tile([P, 8], F32)
         nc.vector.tensor_copy(out=a_par[:], in_=vector_cols[:, 16:24])
         soft = keep.tile([P, 8], F32)
-        nc.scalar.activation(out=soft[:], in_=a_par[:], func=ACT.Abs)
+        nc.scalar.activation(out=soft[:], in_=vector_cols[:, 16:24], func=ACT.Abs)
         nc.scalar.activation(out=soft[:], in_=soft[:], func=ACT.Exp, scale=-1.0)
         nc.scalar.activation(out=soft[:], in_=soft[:], func=ACT.Ln, bias=one[:])
 
@@ -163,13 +170,17 @@ def tile_rglru_t_e_kernel(
         def open_unit(u):
             a_t = a_pool.tile([P, CHANNEL_TILES, BLOCK], F32)
             a_of[u] = a_t
-            result = result_pool.tile([P, ROW_TILES, HEAD], F32)
-            fresh = fresh_pool.tile([P, CHANNEL_TILES, ROW_TILES, P], F32)
-            result_of[u], fresh_of[u] = result, fresh
+            if u < UNITS - 1:
+                result = result_pool.tile([P, ROW_TILES, HEAD], F32)
+                fresh = fresh_pool.tile([P, CHANNEL_TILES, ROW_TILES, P], F32)
+                result_of[u], fresh_of[u] = result, fresh
             root_of[u] = a_t
             if u == UNITS - 1:
                 root_t = a_pool.tile([P, CHANNEL_TILES, BLOCK], F32, tag="a_t")
-                root_of[u] = root_t
+                kept_t = result_pool.tile([P, CHANNEL_TILES, BLOCK], F32, tag="result")
+                new_t = fresh_pool.tile([P, CHANNEL_TILES, BLOCK], F32, tag="fresh")
+                sums_t = a_pool.tile([P, CHANNEL_TILES, ROW_TILES, P], F32, tag="a_t")
+                root_of[u], kept_of[u], new_of[u], sums_out_of[u] = root_t, kept_t, new_t, sums_t
 
         def passes(s):
             u, m = divmod(s, CHANNEL_TILES)
@@ -251,6 +262,53 @@ def tile_rglru_t_e_kernel(
                 op1=ALU.mult,
             )
 
+        def turn_rows(source, channels):
+            turned = turn_pool.tile([P, ROW_TILES, P], BF16, tag="turned")
+            for t in range(ROW_TILES):
+                nc.tensor.transpose(turned[:, t, :], source[:, t, channels], ident_bf16[:])
+            return turned
+
+        def keep_channels(s):
+            u, m = divmod(s, CHANNEL_TILES)
+            b, h = divmod(u, HEADS)
+            state_cols = turn_rows(state_of[b], slice(HEAD * h + P * m, HEAD * h + P * (m + 1)))
+            nc.vector.tensor_tensor(
+                out=kept_of[u][:, m, :],
+                in0=state_cols[:].rearrange("p t r -> p (t r)"),
+                in1=a_of[u][:, m, :],
+                op=ALU.mult,
+            )
+            x_cols = turn_rows(x_of[b][:, h, :, :], slice(P * m, P * (m + 1)))
+            nc.vector.scalar_tensor_tensor(
+                out=new_of[u][:, m, :],
+                in0=tanh_of[s][:],
+                scalar=1.0,
+                in1=x_cols[:].rearrange("p t r -> p (t r)"),
+                op0=ALU.add,
+                op1=ALU.mult,
+            )
+
+        def finish_channels(u, m):
+            b, h = divmod(u, HEADS)
+            new_part = new_of[u][:, m, :]
+            nc.vector.tensor_tensor(out=new_part, in0=root_of[u][:, m, :], in1=new_part, op=ALU.mult)
+            both = turn_pool.tile([P, ROW_TILES, P], F32, tag="turned")
+            for t in range(ROW_TILES):
+                rows = slice(P * t, P * (t + 1))
+                for source, first in ((kept_of[u], True), (new_of[u], False)):
+                    nc.tensor.matmul(
+                        both[:, t, :],
+                        lhsT=source[:, m, rows],
+                        rhs=ident[:],
+                        start=first,
+                        stop=not first,
+                        is_transpose=True,
+                    )
+            part = sums_out_of[u][:, m, :, :]
+            nc.scalar.copy(out=part, in_=both[:])
+            channels = slice(HEAD * h + P * m, HEAD * h + P * (m + 1))
+            nc.sync.dma_start(out=out_blocks[b][:, :, channels], in_=part)
+
         def roots(u):
             for first in range(0, CHANNEL_TILES, ROOT_TILES):
                 root_part = root_of[u][:, first : first + ROOT_TILES, :]
@@ -273,21 +331,6 @@ def tile_rglru_t_e_kernel(
             channels = slice(HEAD * h, HEAD * (h + 1))
             nc.sync.dma_start(out=out_blocks[b][:, tiles, channels], in_=result_of[u][:, tiles, :])
 
-        for u in range(HEADS):
-            for pair in range(ROW_TILES // 2):
-                regroup(u, pair)
-            quantise(u)
-        nc.vector.scalar_tensor_tensor(
-            out=soft[:], in0=a_par[:], scalar=0.0, in1=soft[:], op0=ALU.max, op1=ALU.add
-        )
-        minus_4c = keep.tile([P, 8], F32)
-        nc.vector.tensor_scalar_mul(out=minus_4c[:], in0=soft[:], scalar1=-4.0)
-        load_x(1)
-        load_state(0)
-        for b in range(2, X_BLOCKS):
-            load_x(b)
-        load_state(1)
-
         done = {"passes": 0, "keep": 0, "store": 0, "late": 0}
         late = []
 
@@ -298,12 +341,29 @@ def tile_rglru_t_e_kernel(
 
         def keep_up_to(last):
             for s in range(done["keep"], last + 1):
-                keep_granule(s)
+                (keep_channels if s // CHANNEL_TILES == UNITS - 1 else keep_granule)(s)
                 done["keep"] = s + 1
+
+        minus_4c = keep.tile([P, 8], F32)
+        for u in range(HEADS):
+            for pair in range(ROW_TILES // 2):
+                regroup(u, pair)
+            quantise(u)
+            if u == 0:
+                passes_up_to(0)
+                nc.vector.scalar_tensor_tensor(
+                    out=soft[:], in0=a_par[:], scalar=0.0, in1=soft[:], op0=ALU.max, op1=ALU.add
+                )
+                nc.vector.tensor_scalar_mul(out=minus_4c[:], in0=soft[:], scalar1=-4.0)
+        load_state(0)
+        load_x(1)
+        for b in range(2, X_BLOCKS):
+            load_x(b)
+        load_state(1)
 
         members_of = {}
         regroup_at = {}
-        quantise_at = {4: (2, 3), 6: (4,)}
+        quantise_at = {5: (2, 3), 7: (4,)}
         first = 0
         for r, units in enumerate(ROUNDS):
             members = range(first, first + units)
@@ -317,10 +377,11 @@ def tile_rglru_t_e_kernel(
                 regroup_at[last - (last - start) * (len(pieces) - 1 - i) // len(pieces)] = piece
             if r == 0:
                 for i in range(6):
-                    regroup_at[1 + i] = (2 + i // 2, i % 2)
+                    regroup_at[2 + i] = (2 + i // 2, i % 2)
             first += units
         finished = []
         to_add = []
+        gap_adds = []
         to_square = []
         for s in range(STEPS):
             u, m = divmod(s, CHANNEL_TILES)
@@ -382,6 +443,9 @@ def tile_rglru_t_e_kernel(
                 for v in members[:-1]:
                     for mm in range(CHANNEL_TILES):
                         finish(v, mm)
+                    if v == UNITS - 3:
+                        gap_adds.append(v)
+                        continue
                     add(v, nc.gpsimd)
                     finished.append(v)
                 late.extend([(u, mm) for mm in range(CHANNEL_TILES)])
@@ -389,12 +453,12 @@ def tile_rglru_t_e_kernel(
         square_on_scalar(u, CHANNEL_TILES - 1)
         for v in finished[done["store"] :]:
             store(v)
+        for v in gap_adds:
+            add(v, nc.vector)
+            store(v)
         roots(u)
         for mm in range(CHANNEL_TILES):
-            finish(u, mm)
+            finish_channels(u, mm)
         for v in to_add:
             add(v, nc.vector)
             store(v)
-        for tiles in HALVES:
-            add(u, nc.vector, tiles)
-            store(u, tiles)

@@ -289,7 +289,6 @@ def tile_rglru_t_e_kernel(
             )
 
         def finish_channels(u, m):
-            b, h = divmod(u, HEADS)
             new_part = new_of[u][:, m, :]
             nc.vector.tensor_tensor(out=new_part, in0=root_of[u][:, m, :], in1=new_part, op=ALU.mult)
             both = turn_pool.tile([P, ROW_TILES, P], F32, tag="turned")
@@ -304,14 +303,16 @@ def tile_rglru_t_e_kernel(
                         stop=not first,
                         is_transpose=True,
                     )
-            part = sums_out_of[u][:, m, :, :]
-            nc.scalar.copy(out=part, in_=both[:])
-            channels = slice(HEAD * h + P * m, HEAD * h + P * (m + 1))
-            nc.sync.dma_start(out=out_blocks[b][:, :, channels], in_=part)
+            nc.scalar.copy(out=sums_out_of[u][:, m, :, :], in_=both[:])
 
-        def roots(u):
-            for first in range(0, CHANNEL_TILES, ROOT_TILES):
-                root_part = root_of[u][:, first : first + ROOT_TILES, :]
+        def store_channels(u, m):
+            b, h = divmod(u, HEADS)
+            channels = slice(HEAD * h + P * m, HEAD * h + P * (m + 1))
+            nc.sync.dma_start(out=out_blocks[b][:, :, channels], in_=sums_out_of[u][:, m, :, :])
+
+        def roots(u, width):
+            for first in range(0, CHANNEL_TILES, width):
+                root_part = root_of[u][:, first : first + width, :]
                 nc.scalar.activation(
                     out=root_part, in_=root_part, func=ACT.Sqrt, bias=quarter[:], scale=-0.25
                 )
@@ -381,7 +382,6 @@ def tile_rglru_t_e_kernel(
             first += units
         finished = []
         to_add = []
-        gap_adds = []
         to_square = []
         for s in range(STEPS):
             u, m = divmod(s, CHANNEL_TILES)
@@ -439,12 +439,12 @@ def tile_rglru_t_e_kernel(
                 square(u)
                 passes_up_to(s + 2)
                 for v in members:
-                    roots(v)
+                    roots(v, ROOT_TILES)
                 for v in members[:-1]:
                     for mm in range(CHANNEL_TILES):
                         finish(v, mm)
                     if v == UNITS - 3:
-                        gap_adds.append(v)
+                        add(v, nc.gpsimd, HALVES[0])
                         continue
                     add(v, nc.gpsimd)
                     finished.append(v)
@@ -453,12 +453,15 @@ def tile_rglru_t_e_kernel(
         square_on_scalar(u, CHANNEL_TILES - 1)
         for v in finished[done["store"] :]:
             store(v)
-        for v in gap_adds:
-            add(v, nc.vector)
-            store(v)
-        roots(u)
+        add(u - 2, nc.vector, HALVES[1])
+        store(u - 2)
+        add(u - 1, nc.vector, HALVES[0])
+        store(u - 1, HALVES[0])
+        roots(u, 1)
         for mm in range(CHANNEL_TILES):
             finish_channels(u, mm)
-        for v in to_add:
-            add(v, nc.vector)
-            store(v)
+        add(u - 1, nc.vector, HALVES[1])
+        for mm in range(CHANNEL_TILES):
+            store_channels(u, mm)
+            if mm == ROOT_TILES - 1:
+                store(u - 1, HALVES[1])

from contextlib import ExitStack

import concourse.mybir as mybir
from concourse.masks import make_identity

F32 = mybir.dt.float32
BF16 = mybir.dt.bfloat16
I32 = mybir.dt.int32
U32 = mybir.dt.uint32
U8 = mybir.dt.uint8
FP8X4 = mybir.dt.float8_e4m3fn_x4
ACT = mybir.ActivationFunctionType
ALU = mybir.AluOpType

P = 128
PACK = 4
ROWS = 4096
HEADS = 2
HEAD = 512
CHANNELS = HEADS * HEAD
BLOCK = 512
BLOCKS = ROWS // BLOCK
ROW_TILES = BLOCK // P
CHANNEL_TILES = HEAD // P
GATE_X, GATE_A = 0, 1
ROOT_TILES = 2
UNITS = BLOCKS * HEADS
STEPS = UNITS * CHANNEL_TILES
ROUNDS = (5, 5, 5, 1)
ROUND_UNITS = max(ROUNDS)
X_BLOCKS = 4
STATE_BLOCKS = 2
STORE_STEPS = (1, 3)
ALL_TILES = slice(0, ROW_TILES)
HALVES = (slice(0, ROW_TILES // 2), slice(ROW_TILES // 2, ROW_TILES))

FLOPS = 2 * ROWS * HEAD * HEAD * HEADS * 2


def tile_rglru_t_e_kernel(
    tc, x, state, w_in_words, w_in_scales, b_in, w_a_words, w_a_scales, b_a, a_param, out
):
    nc = tc.nc
    x_blocks = x.rearrange("(b p t) c -> b p t c", p=P, t=ROW_TILES)
    state_blocks = state.rearrange("(b p t) c -> b p t c", p=P, t=ROW_TILES)
    out_blocks = out.rearrange("(b p t) c -> b p t c", p=P, t=ROW_TILES)

    with ExitStack() as ctx:
        keep = ctx.enter_context(tc.tile_pool(name="keep", bufs=1))
        x_pool = ctx.enter_context(tc.tile_pool(name="x", bufs=X_BLOCKS))
        state_pool = ctx.enter_context(tc.tile_pool(name="state", bufs=STATE_BLOCKS))
        grouped_pool = ctx.enter_context(tc.tile_pool(name="grouped", bufs=ROUND_UNITS))
        code_pool = ctx.enter_context(tc.tile_pool(name="codes", bufs=ROUND_UNITS + 1))
        a_pool = ctx.enter_context(tc.tile_pool(name="a", bufs=ROUND_UNITS + 1))
        tanh_pool = ctx.enter_context(tc.tile_pool(name="tanh", bufs=3))
        result_pool = ctx.enter_context(tc.tile_pool(name="result", bufs=ROUND_UNITS + 1))
        fresh_pool = ctx.enter_context(tc.tile_pool(name="fresh", bufs=ROUND_UNITS))
        sum_pool = ctx.enter_context(tc.psum_pool(name="sums", bufs=4))
        turn_pool = ctx.enter_context(tc.psum_pool(name="turned", bufs=4))
        ctx.enter_context(tc.manual_schedule())

        x_of, state_of = {}, {}
        grouped_of, codes_of, planes_of = {}, {}, {}
        a_of, root_of, result_of, fresh_of = {}, {}, {}, {}
        sums_of, tanh_of = {}, {}
        kept_of, new_of, sums_out_of = {}, {}, {}

        def load_x_head(b, h):
            channels = slice(HEAD * h, HEAD * (h + 1))
            nc.sync.dma_start(out=x_of[b][:, h, :, :], in_=x_blocks[b][:, :, channels])

        def load_x(b):
            x_sb = x_pool.tile([P, HEADS, ROW_TILES, HEAD], BF16)
            x_of[b] = x_sb
            for h in range(HEADS):
                load_x_head(b, h)

        def load_state(b):
            state_sb = state_pool.tile([P, ROW_TILES, CHANNELS], BF16)
            nc.sync.dma_start(out=state_sb[:], in_=state_blocks[b])
            state_of[b] = state_sb

        x_first = x_pool.tile([P, HEADS, ROW_TILES, HEAD], BF16, tag="x_sb")
        x_of[0] = x_first
        load_x_head(0, 0)
        ident = keep.tile([P, P], F32)
        make_identity(nc, ident[:])
        ident_bf16 = keep.tile([P, P], BF16)
        make_identity(nc, ident_bf16[:])
        vector_rows = keep.tile([P, P], BF16)
        nc.vector.memset(vector_rows[:], 0.0)
        w_planes = keep.tile([P, 2 * HEADS, HEAD], U8, align_bytes=64)
        nc.vector.memset(w_planes[:].bitcast(I32), 0)
        quarter = keep.tile([P, 1], F32)
        nc.vector.memset(quarter[:], 0.25)
        last_code = keep.tile([P, 1], U32)
        one = keep.tile([P, 1], F32)
        nc.vector.memset(one[:], 1.0)

        nc.sync.dma_start(out=vector_rows[0:8, :], in_=b_in.rearrange("h (m p) -> (h m) p", p=P))
        nc.sync.dma_start(out=vector_rows[8:16, :], in_=b_a.rearrange("h (m p) -> (h m) p", p=P))
        nc.sync.dma_start(out=vector_rows[16:24, :], in_=a_param.rearrange("(m p) -> m p", p=P))
        w_codes = keep.tile([P, 2 * HEADS, HEAD], I32, align_bytes=64)

        def load_weights(h):
            for gate, words in ((GATE_A, w_a_words), (GATE_X, w_in_words)):
                nc.sync.dma_start(
                    out=w_codes[:, HEADS * gate + h, :],
                    in_=words[h].rearrange("p n t -> p (n t)").bitcast(I32),
                )

        load_weights(0)
        for gate, scales in ((GATE_X, w_in_scales), (GATE_A, w_a_scales)):
            for quadrant in range(4):
                nc.sync.dma_start(
                    out=w_planes[
                        32 * quadrant : 32 * quadrant + 4, HEADS * gate : HEADS * (gate + 1), :
                    ].bitcast(I32),
                    in_=scales[:, 4 * quadrant : 4 * quadrant + 4, :]
                    .rearrange("g r n -> r g n")
                    .bitcast(I32),
                )

        load_x_head(0, 1)
        load_weights(1)

        vector_cols = turn_pool.tile([P, P], BF16, tag="turned")
        nc.tensor.transpose(vector_cols[:], vector_rows[:], ident_bf16[:])
        half_bias = keep.tile([P, 16], F32)
        nc.vector.tensor_scalar_mul(out=half_bias[:], in0=vector_cols[:, 0:16], scalar1=0.5)
        a_par = keep.tile([P, 8], F32)
        nc.vector.tensor_copy(out=a_par[:], in_=vector_cols[:, 16:24])
        soft = keep.tile([P, 8], F32)
        nc.scalar.activation(out=soft[:], in_=vector_cols[:, 16:24], func=ACT.Abs)
        nc.scalar.activation(out=soft[:], in_=soft[:], func=ACT.Exp, scale=-1.0)
        nc.scalar.activation(out=soft[:], in_=soft[:], func=ACT.Ln, bias=one[:])

        def regroup(u, pair):
            if pair == 0:
                grouped = grouped_pool.tile([P, BLOCK, PACK], BF16, align_bytes=64)
                grouped_of[u] = grouped
            b, h = divmod(u, HEADS)
            x_words = x_of[b][:].bitcast(F32)
            grouped_words = grouped_of[u][:].bitcast(F32)
            turned = turn_pool.tile([P, 2, 2, P], F32, tag="turned")
            for i in range(2):
                for w in range(2):
                    nc.tensor.transpose(
                        turned[:, i, w, :],
                        x_words[:, h, 2 * pair + i, w : HEAD // 2 : 2],
                        ident[:],
                    )
            nc.vector.tensor_copy(
                out=grouped_words[:, 2 * P * pair : 2 * P * (pair + 1), :].rearrange(
                    "p (i r) w -> p i r w", i=2
                ),
                in_=turned[:].rearrange("p i w r -> p i r w"),
            )

        def quantise(u):
            codes = code_pool.tile([P, BLOCK], U32, align_bytes=64)
            plane = code_pool.tile([P, BLOCK], U8, align_bytes=64)
            codes_of[u], planes_of[u] = codes, plane
            nc.vector.quantize_mx(
                out=codes[:].bitcast(FP8X4),
                scales=plane[:],
                in_=grouped_of[u][:].rearrange("p r t -> p (r t)"),
            )

        def open_unit(u):
            a_t = a_pool.tile([P, CHANNEL_TILES, BLOCK], F32)
            a_of[u] = a_t
            if u < UNITS - 1:
                result = result_pool.tile([P, ROW_TILES, HEAD], F32)
                fresh = fresh_pool.tile([P, CHANNEL_TILES, ROW_TILES, P], F32)
                result_of[u], fresh_of[u] = result, fresh
            root_of[u] = a_t
            if u == UNITS - 1:
                root_t = a_pool.tile([P, CHANNEL_TILES, BLOCK], F32, tag="a_t")
                kept_t = result_pool.tile([P, CHANNEL_TILES, BLOCK], F32, tag="result")
                new_t = fresh_pool.tile([P, CHANNEL_TILES, BLOCK], F32, tag="fresh")
                sums_t = a_pool.tile([P, CHANNEL_TILES, ROW_TILES, P], F32, tag="a_t")
                root_of[u], kept_of[u], new_of[u], sums_out_of[u] = root_t, kept_t, new_t, sums_t

        def passes(s):
            u, m = divmod(s, CHANNEL_TILES)
            h = u % HEADS
            channels = slice(P * m, P * (m + 1))
            for gate in (GATE_A, GATE_X):
                acc = sum_pool.tile([P, BLOCK], F32)
                nc.tensor.matmul_mx(
                    out=acc[:],
                    lhsT=w_codes[:, HEADS * gate + h, channels].bitcast(FP8X4),
                    lhsT_scale=w_planes[:, HEADS * gate + h, channels],
                    rhs=codes_of[u][:].bitcast(FP8X4),
                    rhs_scale=planes_of[u][:],
                    start=True,
                    stop=True,
                )
                sums_of[s, gate] = acc

        def gates(s):
            u, m = divmod(s, CHANNEL_TILES)
            column = CHANNEL_TILES * (u % HEADS) + m
            a_part = a_of[u][:, m, :]
            tanh_t = tanh_pool.tile([P, BLOCK], F32)
            for gate, target in ((GATE_A, a_part), (GATE_X, tanh_t[:])):
                nc.scalar.activation(
                    out=target,
                    in_=sums_of[s, gate][:],
                    func=ACT.Tanh,
                    bias=half_bias[:, 8 * gate + column : 8 * gate + column + 1],
                    scale=0.5,
                )
            nc.scalar.activation(
                out=a_part,
                in_=a_part,
                func=ACT.Exp,
                bias=minus_4c[:, column : column + 1],
                scale=minus_4c[:, column : column + 1],
            )
            tanh_of[s] = tanh_t

        def square(u):
            nc.gpsimd.tensor_tensor(out=root_of[u][:], in0=a_of[u][:], in1=a_of[u][:], op=ALU.mult)

        def follow_quantise(u):
            nc.gpsimd.tensor_copy(out=last_code[:], in_=codes_of[u][:, 0:1])

        def square_on_scalar(u, m):
            nc.scalar.activation(out=root_of[u][:, m, :], in_=a_of[u][:, m, :], func=ACT.Square)

        def square_granule(u, m):
            part = a_of[u][:, m, :]
            nc.gpsimd.tensor_tensor(out=root_of[u][:, m, :], in0=part, in1=part, op=ALU.mult)

        def turn_back(source):
            turned = turn_pool.tile([P, ROW_TILES, P], F32, tag="turned")
            for t in range(ROW_TILES):
                nc.tensor.transpose(turned[:, t, :], source[:, P * t : P * (t + 1)], ident[:])
            return turned

        def keep_granule(s):
            u, m = divmod(s, CHANNEL_TILES)
            b, h = divmod(u, HEADS)
            inside = slice(P * m, P * (m + 1))
            channels = slice(HEAD * h + P * m, HEAD * h + P * (m + 1))
            a_rows = turn_back(a_of[u][:, m, :])
            nc.vector.tensor_tensor(
                out=result_of[u][:, :, inside],
                in0=a_rows[:],
                in1=state_of[b][:, :, channels],
                op=ALU.mult,
            )
            tanh_rows = turn_back(tanh_of[s])
            nc.vector.scalar_tensor_tensor(
                out=fresh_of[u][:, m, :, :],
                in0=tanh_rows[:],
                scalar=1.0,
                in1=x_of[b][:, h, :, inside],
                op0=ALU.add,
                op1=ALU.mult,
            )

        def turn_rows(source, channels):
            turned = turn_pool.tile([P, ROW_TILES, P], BF16, tag="turned")
            for t in range(ROW_TILES):
                nc.tensor.transpose(turned[:, t, :], source[:, t, channels], ident_bf16[:])
            return turned

        def keep_channels(s):
            u, m = divmod(s, CHANNEL_TILES)
            b, h = divmod(u, HEADS)
            state_cols = turn_rows(state_of[b], slice(HEAD * h + P * m, HEAD * h + P * (m + 1)))
            nc.vector.tensor_tensor(
                out=kept_of[u][:, m, :],
                in0=state_cols[:].rearrange("p t r -> p (t r)"),
                in1=a_of[u][:, m, :],
                op=ALU.mult,
            )
            x_cols = turn_rows(x_of[b][:, h, :, :], slice(P * m, P * (m + 1)))
            nc.vector.scalar_tensor_tensor(
                out=new_of[u][:, m, :],
                in0=tanh_of[s][:],
                scalar=1.0,
                in1=x_cols[:].rearrange("p t r -> p (t r)"),
                op0=ALU.add,
                op1=ALU.mult,
            )

        def finish_channels(u, m):
            new_part = new_of[u][:, m, :]
            nc.vector.tensor_tensor(out=new_part, in0=root_of[u][:, m, :], in1=new_part, op=ALU.mult)
            both = turn_pool.tile([P, ROW_TILES, P], F32, tag="turned")
            for t in range(ROW_TILES):
                rows = slice(P * t, P * (t + 1))
                for source, first in ((kept_of[u], True), (new_of[u], False)):
                    nc.tensor.matmul(
                        both[:, t, :],
                        lhsT=source[:, m, rows],
                        rhs=ident[:],
                        start=first,
                        stop=not first,
                        is_transpose=True,
                    )
            nc.scalar.copy(out=sums_out_of[u][:, m, :, :], in_=both[:])

        def store_channels(u, m):
            b, h = divmod(u, HEADS)
            channels = slice(HEAD * h + P * m, HEAD * h + P * (m + 1))
            nc.sync.dma_start(out=out_blocks[b][:, :, channels], in_=sums_out_of[u][:, m, :, :])

        def roots(u, width):
            for first in range(0, CHANNEL_TILES, width):
                root_part = root_of[u][:, first : first + width, :]
                nc.scalar.activation(
                    out=root_part, in_=root_part, func=ACT.Sqrt, bias=quarter[:], scale=-0.25
                )

        def finish(u, m):
            root_rows = turn_back(root_of[u][:, m, :])
            fresh_part = fresh_of[u][:, m, :, :]
            nc.vector.tensor_tensor(out=fresh_part, in0=root_rows[:], in1=fresh_part, op=ALU.mult)

        def add(u, adder, tiles=ALL_TILES):
            part = result_of[u][:, tiles, :].rearrange("p t (m c) -> p t m c", c=P)
            fresh_part = fresh_of[u][:, :, tiles, :].rearrange("p m t c -> p t m c")
            adder.tensor_tensor(out=part, in0=part, in1=fresh_part, op=ALU.add)

        def store(u, tiles=ALL_TILES):
            b, h = divmod(u, HEADS)
            channels = slice(HEAD * h, HEAD * (h + 1))
            nc.sync.dma_start(out=out_blocks[b][:, tiles, channels], in_=result_of[u][:, tiles, :])

        done = {"passes": 0, "keep": 0, "store": 0, "late": 0}
        late = []

        def passes_up_to(last):
            for s in range(done["passes"], min(last, STEPS - 1) + 1):
                passes(s)
                done["passes"] = s + 1

        def keep_up_to(last):
            for s in range(done["keep"], last + 1):
                (keep_channels if s // CHANNEL_TILES == UNITS - 1 else keep_granule)(s)
                done["keep"] = s + 1

        minus_4c = keep.tile([P, 8], F32)
        for u in range(HEADS):
            for pair in range(ROW_TILES // 2):
                regroup(u, pair)
            quantise(u)
            if u == 0:
                passes_up_to(0)
                nc.vector.scalar_tensor_tensor(
                    out=soft[:], in0=a_par[:], scalar=0.0, in1=soft[:], op0=ALU.max, op1=ALU.add
                )
                nc.vector.tensor_scalar_mul(out=minus_4c[:], in0=soft[:], scalar1=-4.0)
        load_state(0)
        load_x(1)
        for b in range(2, X_BLOCKS):
            load_x(b)
        load_state(1)

        members_of = {}
        regroup_at = {}
        quantise_at = {5: (2, 3), 7: (4,)}
        first = 0
        for r, units in enumerate(ROUNDS):
            members = range(first, first + units)
            for u in members:
                members_of[u] = members
            following = range(members.stop, members.stop + ROUNDS[r + 1]) if r + 1 < len(ROUNDS) else ()
            pieces = [(u, pair) for u in following for pair in range(ROW_TILES // 2)]
            last = CHANNEL_TILES * members.stop - 2
            start = max(CHANNEL_TILES * first, 8)
            for i, piece in enumerate(pieces):
                regroup_at[last - (last - start) * (len(pieces) - 1 - i) // len(pieces)] = piece
            if r == 0:
                for i in range(6):
                    regroup_at[2 + i] = (2 + i // 2, i % 2)
            first += units
        finished = []
        to_add = []
        to_square = []
        for s in range(STEPS):
            u, m = divmod(s, CHANNEL_TILES)
            members = members_of[u]
            round_end = s == CHANNEL_TILES * members.stop - 1
            last_round = members.stop == UNITS
            if m == 0:
                open_unit(u)
            passes_up_to(min(s + 1, CHANNEL_TILES * members.stop - 1))
            gates(s)
            if last_round and m > 0:
                square_on_scalar(u, m - 1)
            if round_end and not last_round:
                following = members_of[u + 1] if u + 1 in members_of else ()
                for v in following:
                    quantise(v)
                follow_quantise(following[-1])
            keep_up_to(s - 1)
            if done["late"] < len(late):
                v, mm = late[done["late"]]
                done["late"] += 1
                finish(v, mm)
                if mm == CHANNEL_TILES - 1:
                    to_add.append(v)
            if s in regroup_at:
                regroup(*regroup_at[s])
            for v in quantise_at.get(s, ()):
                quantise(v)
            b, h = divmod(u, HEADS)
            if h == 0 and m == 0 and b >= 1:
                if b - 1 + X_BLOCKS < BLOCKS:
                    load_x(b - 1 + X_BLOCKS)
                if b - 1 + STATE_BLOCKS < BLOCKS:
                    load_state(b - 1 + STATE_BLOCKS)
            if m in STORE_STEPS and done["store"] < len(finished):
                store(finished[done["store"]])
                done["store"] += 1
            if m == 0 and to_square:
                square(to_square.pop())
            if s in range(1, CHANNEL_TILES):
                square_granule(u, m - 1)
            if s == CHANNEL_TILES:
                square_granule(0, m + CHANNEL_TILES - 1)
            if not last_round:
                for v in to_add:
                    add(v, nc.gpsimd)
                finished.extend(to_add)
                to_add.clear()
            if m == CHANNEL_TILES - 1 and not round_end and u > 0:
                to_square.append(u)
            if round_end:
                keep_up_to(s)
                if last_round:
                    continue
                square(u)
                passes_up_to(s + 2)
                for v in members:
                    roots(v, ROOT_TILES)
                for v in members[:-1]:
                    for mm in range(CHANNEL_TILES):
                        finish(v, mm)
                    if v == UNITS - 3:
                        add(v, nc.gpsimd, HALVES[0])
                        continue
                    add(v, nc.gpsimd)
                    finished.append(v)
                late.extend([(u, mm) for mm in range(CHANNEL_TILES)])
        u = UNITS - 1
        square_on_scalar(u, CHANNEL_TILES - 1)
        for v in finished[done["store"] :]:
            store(v)
        add(u - 2, nc.vector, HALVES[1])
        store(u - 2)
        add(u - 1, nc.vector, HALVES[0])
        store(u - 1, HALVES[0])
        roots(u, 1)
        for mm in range(CHANNEL_TILES):
            finish_channels(u, mm)
        add(u - 1, nc.vector, HALVES[1])
        for mm in range(CHANNEL_TILES):
            store_channels(u, mm)
            if mm == ROOT_TILES - 1:
                store(u - 1, HALVES[1])
